import numpy as np
import ml_dtypes


def mxq(x, axis, fmt="e4m3"):
    dtype, down = {"e4m3": (ml_dtypes.float8_e4m3fn, 7), "e5m2": (ml_dtypes.float8_e5m2, 14)}[fmt]
    v = np.moveaxis(np.asarray(x, np.float32).astype(ml_dtypes.bfloat16).astype(np.float64), axis, -1)
    blocks = v.reshape(v.shape[:-1] + (-1, 32))
    amax = np.abs(blocks).max(-1, keepdims=True)
    byte = np.maximum(np.where(amax > 0, np.frexp(amax)[1] - 1 + 127, 0) - down, 1)
    scale = np.exp2(byte - 127.0)
    codes = (blocks / scale).astype(np.float32).astype(dtype).astype(np.float64)
    return np.moveaxis((codes * scale).reshape(v.shape), -1, axis)


WIDE = False


def mx_kscale(k):
    if not WIDE:
        return np.ones(k)
    levels = np.array([10, -10, 5, -5, 0])
    a = np.random.permutation(np.resize(levels, k // 512 * 4)).reshape(k // 512, 4)
    idx = np.arange(k)
    return np.exp2(a[idx // 512, idx % 128 // 32])


BF16 = ml_dtypes.bfloat16


def bf(x):
    return np.asarray(x, np.float32).astype(BF16)


def f64(x):
    return np.asarray(x).astype(np.float64)


B, DIM, HID, H, SEQ, DOUT = 128, 1024, 128, 8, 1024, 512
DECAY_CONSTANT = SEQ // 512
H2 = H // 2
F = H * HID


def setup_inputs():
    s = mx_kscale(DIM)
    x = bf(np.random.standard_normal((B, DIM)) * s)
    W_proj = bf(np.random.standard_normal((H, DIM, HID)) / np.sqrt(DIM) / s[:, None])
    b_proj = bf(np.random.standard_normal((H, HID)) * 0.1)
    W_out = bf(np.random.standard_normal((F, DOUT)) / np.sqrt(F))
    b_out = bf(np.random.standard_normal(DOUT) * 0.1)
    w_mix = bf(np.concatenate([0.4 + 0.05 * np.random.standard_normal((H2, SEQ)), -0.3 + 0.05 * np.random.standard_normal((H - H2, SEQ))], axis=0))
    b_mix = bf(np.concatenate([3.0 + 0.1 * np.random.standard_normal((H2, SEQ)), 0.2 + 0.1 * np.random.standard_normal((H - H2, SEQ))], axis=0))
    decay_values = bf(0.95 + 0.05 * np.random.standard_normal(H))
    caches = bf(np.random.standard_normal((H, B, HID)))
    return {"x": x, "index": 7, "W_proj": W_proj, "b_proj": b_proj, "W_out": W_out, "b_out": b_out,
            "w_mix": w_mix, "b_mix": b_mix, "decay_values": decay_values, "caches": caches}


def reference(x, index, W_proj, b_proj, W_out, b_out, w_mix, b_mix, decay_values, caches):
    proj = (mxq(f64(x), 1, "e4m3") @ mxq(f64(W_proj), 1, "e4m3")) + f64(b_proj)[:, None, :]
    decay = np.clip(f64(decay_values), 0.9, 1.0) ** (1.0 / DECAY_CONSTANT)
    w = f64(w_mix)[:, index]
    b = f64(b_mix)[:, index]
    cache_coef = np.concatenate([w[:H2] * decay[:H2], decay[H2:]], axis=0)
    out = (w[:, None, None] * proj
           + cache_coef[:, None, None] * f64(caches)
           + b[:, None, None])
    hidden = np.transpose(out, (1, 0, 2)).reshape(B, H * HID)
    return (mxq(hidden, 1, "e4m3") @ mxq(f64(W_out), 0, "e4m3")) + f64(b_out)

@@ -1,0 +1,219 @@
+from contextlib import ExitStack
+
+import concourse.mybir as mybir
+from concourse.masks import make_identity
+
+F32 = mybir.dt.float32
+BF16 = mybir.dt.bfloat16
+U32 = mybir.dt.uint32
+U8 = mybir.dt.uint8
+FP8X4 = mybir.dt.float8_e4m3fn_x4
+ALU = mybir.AluOpType
+ACT = mybir.ActivationFunctionType
+
+P = 128
+PACK = 4
+K_PASS = P * PACK
+B, DIM, HID, H, DOUT = 128, 1024, 128, 8, 512
+H2 = H // 2
+DECAY_CONSTANT = 2
+PASSES = DIM // K_PASS
+RUN = 4
+HALF = DOUT // 2
+
+W_AT, B_AT, DECAY_AT, SMALL = 0, 16, 32, 64
+
+FLOPS = 2 * B * DIM * H * HID + 2 * B * H * HID * DOUT
+
+
+def regroup(copy, grouped, rows):
+    copy(
+        out=grouped.rearrange("p (a i) j -> p a j i", i=RUN),
+        in_=rows.rearrange("p j (a i) -> p a j i", i=RUN),
+    )
+
+
+def tile_mixedrepeatheads_s_kernel(
+    tc, x, index, W_proj, b_proj, W_out, b_out, w_mix, b_mix, decay_values, caches, out
+):
+    nc = tc.nc
+    with ExitStack() as ctx:
+        keep = ctx.enter_context(tc.tile_pool(name="keep", bufs=1))
+        psum = ctx.enter_context(tc.psum_pool(name="psum", bufs=1))
+
+        x_sb = keep.tile([P, DIM], BF16)
+        nc.sync.dma_start(out=x_sb[:], in_=x)
+
+        wp_rows = [keep.tile([P, PASSES, PACK, HID], BF16, name="wp_rows%d" % h) for h in range(H)]
+        caches_sb = keep.tile([P, H, HID], BF16)
+        for h in range(H):
+            if h == H2:
+                nc.sync.dma_start(out=caches_sb[:], in_=caches.rearrange("h r k -> r h k"))
+            nc.sync.dma_start(
+                out=wp_rows[h][:].rearrange("p c j n -> p c (j n)"),
+                in_=W_proj[h].rearrange("(c p j) n -> p c (j n)", c=PASSES, p=P, j=PACK),
+            )
+
+        wo_rows = [keep.tile([P, PACK, DOUT], BF16, name="wo_rows%d" % g) for g in range(PASSES)]
+        wo_view = W_out.rearrange("(g t p) n -> g p t n", g=PASSES, t=PACK, p=P)
+        for g in range(PASSES):
+            nc.sync.dma_start(out=wo_rows[g][:], in_=wo_view[g])
+
+        bout_row = keep.tile([P, DOUT], BF16)
+        small_row = keep.tile([P, SMALL], BF16)
+        bproj_rows = keep.tile([P, P], BF16)
+        nc.vector.memset(bout_row[:], 0.0)
+        nc.vector.memset(small_row[:], 0.0)
+        nc.vector.memset(bproj_rows[:], 0.0)
+        nc.scalar.dma_start(out=bout_row[0:1, :], in_=b_out.rearrange("(o n) -> o n", o=1))
+        nc.scalar.dma_start(out=bproj_rows[0:H, :], in_=b_proj)
+        nc.scalar.dma_start(
+            out=small_row[0:1, DECAY_AT : DECAY_AT + H],
+            in_=decay_values.rearrange("(o h) -> o h", o=1),
+        )
+        with nc.allow_non_contiguous_dma(reason="column index of w_mix and b_mix: 8 elements each"):
+            nc.scalar.dma_start(
+                out=small_row[0:1, W_AT : W_AT + H],
+                in_=w_mix[:, index : index + 1].rearrange("h o -> o h"),
+            )
+            nc.scalar.dma_start(
+                out=small_row[0:1, B_AT : B_AT + H],
+                in_=b_mix[:, index : index + 1].rearrange("h o -> o h"),
+            )
+
+        ident_f32 = keep.tile([P, P], F32)
+        make_identity(nc, ident_f32[:])
+        ones = keep.tile([P, P], BF16)
+        nc.gpsimd.memset(ones[:], 1.0)
+        ident_bf16 = keep.tile([P, P], BF16)
+        make_identity(nc, ident_bf16[:])
+        exponent = keep.tile([P, H], F32)
+        nc.gpsimd.memset(exponent[:], 1.0 / DECAY_CONSTANT)
+
+        x_words = x_sb[:].bitcast(F32).rearrange("r (c p u) -> r c u p", c=PASSES, p=P, u=2)
+        xT = psum.tile([P, PASSES, 2, B], F32)
+        for c in range(PASSES):
+            for u in range(2):
+                nc.tensor.transpose(xT[:, c, u, :], x_words[:, c, u, :], ident_f32[:])
+        x_grouped = keep.tile([P, PASSES * B * PACK], BF16, align_bytes=64)
+        nc.scalar.copy(
+            out=x_grouped[:].bitcast(F32).rearrange("p (c r u) -> p c r u", c=PASSES, r=B, u=2),
+            in_=xT[:].rearrange("p c u r -> p c r u"),
+        )
+        x_codes = keep.tile([P, PASSES, B], U32, align_bytes=64)
+        x_scales = keep.tile([P, PASSES, B], U8, align_bytes=64)
+        nc.vector.quantize_mx(
+            out=x_codes[:].rearrange("p c r -> p (c r)").bitcast(FP8X4),
+            scales=x_scales[:].rearrange("p c r -> p (c r)"),
+            in_=x_grouped[:],
+        )
+
+        bout_ps = psum.tile([P, DOUT], F32)
+        nc.tensor.matmul(bout_ps[:], lhsT=ones[:], rhs=bout_row[:], start=True, stop=True)
+        bout_all = keep.tile([P, DOUT], F32)
+        nc.scalar.copy(out=bout_all[:], in_=bout_ps[:])
+
+        small_ps = psum.tile([P, SMALL], F32)
+        nc.tensor.matmul(small_ps[:], lhsT=ones[:], rhs=small_row[:], start=True, stop=True)
+        small_all = keep.tile([P, SMALL], F32)
+        nc.vector.tensor_copy(out=small_all[:], in_=small_ps[:])
+        w_all = small_all[:, W_AT : W_AT + H]
+        b_all = small_all[:, B_AT : B_AT + H]
+
+        coef = keep.tile([P, H], F32)
+        nc.gpsimd.tensor_scalar(
+            out=coef[:], in0=small_all[:, DECAY_AT : DECAY_AT + H],
+            scalar1=0.9, scalar2=1.0, op0=ALU.max, op1=ALU.min,
+        )
+        nc.gpsimd.tensor_tensor(out=coef[:], in0=coef[:], in1=exponent[:], op=ALU.pow)
+        nc.gpsimd.tensor_tensor(out=coef[:, 0:H2], in0=coef[:, 0:H2], in1=w_all[:, 0:H2], op=ALU.mult)
+
+        bprojT = psum.tile([P, P], BF16)
+        nc.tensor.transpose(bprojT[:], bproj_rows[:], ident_bf16[:])
+        shift = keep.tile([P, H], F32)
+        nc.vector.tensor_tensor(out=shift[:], in0=bprojT[:, 0:H], in1=w_all, op=ALU.mult)
+        nc.vector.tensor_tensor(out=shift[:], in0=shift[:], in1=b_all, op=ALU.add)
+
+        wp_grouped = [keep.tile([P, PASSES, HID, PACK], BF16, name="wp_grouped%d" % h, align_bytes=64) for h in range(H)]
+        wp_codes = [keep.tile([P, PASSES, HID], U32, name="wp_codes%d" % h, align_bytes=64) for h in range(H)]
+        wp_scales = [keep.tile([P, PASSES, HID], U8, name="wp_scales%d" % h, align_bytes=64) for h in range(H)]
+        projT = [psum.tile([P, PACK, B], F32, name="projT%d" % g) for g in range(PASSES)]
+        cachesT = psum.tile([P, H, B], BF16)
+        rest = keep.tile([P, H, B], F32)
+        hid = [keep.tile([P, PACK, B], BF16, name="hid%d" % g) for g in range(PASSES)]
+        hid_grouped = [keep.tile([P, B, PACK], BF16, name="hid_grouped%d" % g, align_bytes=64) for g in range(PASSES)]
+        hid_codes = [keep.tile([P, B], U32, name="hid_codes%d" % g, align_bytes=64) for g in range(PASSES)]
+        hid_scales = [keep.tile([P, B], U8, name="hid_scales%d" % g, align_bytes=64) for g in range(PASSES)]
+
+        for g in range(PASSES):
+            for t in range(PACK):
+                h = PACK * g + t
+                copy = nc.vector.tensor_copy if h % 2 == 0 else nc.scalar.copy
+                for c in range(PASSES):
+                    regroup(copy, wp_grouped[h][:, c], wp_rows[h][:, c])
+                nc.vector.quantize_mx(
+                    out=wp_codes[h][:].rearrange("p c n -> p (c n)").bitcast(FP8X4),
+                    scales=wp_scales[h][:].rearrange("p c n -> p (c n)"),
+                    in_=wp_grouped[h][:].rearrange("p c n j -> p (c n j)"),
+                )
+                for c in range(PASSES):
+                    nc.tensor.matmul_mx(
+                        out=projT[g][:, t, :],
+                        lhsT=wp_codes[h][:, c, :].bitcast(FP8X4),
+                        lhsT_scale=wp_scales[h][:, c, :],
+                        rhs=x_codes[:, c, :].bitcast(FP8X4),
+                        rhs_scale=x_scales[:, c, :],
+                        start=(c == 0),
+                        stop=(c == PASSES - 1),
+                    )
+
+            if g == 0:
+                for h in range(H):
+                    nc.tensor.transpose(cachesT[:, h, :], caches_sb[:, h, :], ident_bf16[:])
+                for h in range(H):
+                    nc.scalar.activation(
+                        out=rest[:, h, :], in_=cachesT[:, h, :], func=ACT.Identity,
+                        scale=coef[:, h : h + 1], bias=shift[:, h : h + 1],
+                    )
+
+            for t in range(PACK):
+                h = PACK * g + t
+                nc.vector.scalar_tensor_tensor(
+                    out=hid[g][:, t, :], in0=projT[g][:, t, :], scalar=w_all[:, h : h + 1],
+                    in1=rest[:, h, :], op0=ALU.mult, op1=ALU.add,
+                )
+            regroup(nc.vector.tensor_copy, hid_grouped[g][:], hid[g][:])
+            nc.vector.quantize_mx(
+                out=hid_codes[g][:].bitcast(FP8X4),
+                scales=hid_scales[g][:],
+                in_=hid_grouped[g][:].rearrange("p r t -> p (r t)"),
+            )
+
+        wo_grouped = [keep.tile([P, DOUT, PACK], BF16, name="wo_grouped%d" % g, align_bytes=64) for g in range(PASSES)]
+        wo_codes = [keep.tile([P, DOUT], U32, name="wo_codes%d" % g, align_bytes=64) for g in range(PASSES)]
+        wo_scales = [keep.tile([P, DOUT], U8, name="wo_scales%d" % g, align_bytes=64) for g in range(PASSES)]
+        acc = psum.tile([P, DOUT], F32)
+        for g in range(PASSES):
+            for half, copy in enumerate((nc.vector.tensor_copy, nc.scalar.copy)):
+                cols = slice(half * HALF, (half + 1) * HALF)
+                regroup(copy, wo_grouped[g][:, cols, :], wo_rows[g][:, :, cols])
+            for half in range(2):
+                cols = slice(half * HALF, (half + 1) * HALF)
+                nc.vector.quantize_mx(
+                    out=wo_codes[g][:, cols].bitcast(FP8X4),
+                    scales=wo_scales[g][:, cols],
+                    in_=wo_grouped[g][:, cols, :].rearrange("p n j -> p (n j)"),
+                )
+            nc.tensor.matmul_mx(
+                out=acc[:],
+                lhsT=hid_codes[g][:].bitcast(FP8X4),
+                lhsT_scale=hid_scales[g][:],
+                rhs=wo_codes[g][:].bitcast(FP8X4),
+                rhs_scale=wo_scales[g][:],
+                start=(g == 0),
+                stop=(g == PASSES - 1),
+            )
+
+        result = keep.tile([P, DOUT], F32)
+        nc.vector.tensor_tensor(out=result[:], in0=acc[:], in1=bout_all[:], op=ALU.add)
+        nc.sync.dma_start(out=out, in_=result[:])

@@ -16,10 +16,11 @@ PACK = 4
 K_PASS = P * PACK
 B, DIM, HID, H, DOUT = 128, 1024, 128, 8, 512
 H2 = H // 2
-DECAY_CONSTANT = 2
 PASSES = DIM // K_PASS
 RUN = 4
 HALF = DOUT // 2
+ROWS_PP = H * B // P
+PARTS_PH = P // H
 
 W_AT, B_AT, DECAY_AT, SMALL = 0, 16, 32, 64
 
@@ -40,24 +41,6 @@ def tile_mixedrepeatheads_s_kernel(
     with ExitStack() as ctx:
         keep = ctx.enter_context(tc.tile_pool(name="keep", bufs=1))
         psum = ctx.enter_context(tc.psum_pool(name="psum", bufs=1))
-
-        x_sb = keep.tile([P, DIM], BF16)
-        nc.sync.dma_start(out=x_sb[:], in_=x)
-
-        wp_rows = [keep.tile([P, PASSES, PACK, HID], BF16, name="wp_rows%d" % h) for h in range(H)]
-        caches_sb = keep.tile([P, H, HID], BF16)
-        for h in range(H):
-            if h == H2:
-                nc.sync.dma_start(out=caches_sb[:], in_=caches.rearrange("h r k -> r h k"))
-            nc.sync.dma_start(
-                out=wp_rows[h][:].rearrange("p c j n -> p c (j n)"),
-                in_=W_proj[h].rearrange("(c p j) n -> p c (j n)", c=PASSES, p=P, j=PACK),
-            )
-
-        wo_rows = [keep.tile([P, PACK, DOUT], BF16, name="wo_rows%d" % g) for g in range(PASSES)]
-        wo_view = W_out.rearrange("(g t p) n -> g p t n", g=PASSES, t=PACK, p=P)
-        for g in range(PASSES):
-            nc.sync.dma_start(out=wo_rows[g][:], in_=wo_view[g])
 
         bout_row = keep.tile([P, DOUT], BF16)
         small_row = keep.tile([P, SMALL], BF16)
@@ -81,17 +64,38 @@ def tile_mixedrepeatheads_s_kernel(
                 in_=b_mix[:, index : index + 1].rearrange("h o -> o h"),
             )
 
+        x_sb = keep.tile([P, DIM], BF16)
+        wp_rows = [keep.tile([P, PASSES, PACK, HID], BF16, name="wp_rows%d" % h) for h in range(H)]
+        caches_sb = keep.tile([P, ROWS_PP, HID], BF16)
+        for h in range(H):
+            if h == 2:
+                nc.sync.dma_start(out=x_sb[:], in_=x)
+                nc.sync.dma_start(
+                    out=caches_sb[:].rearrange("p j k -> p (j k)"),
+                    in_=caches.rearrange("h r k -> (h r) k").rearrange("(p j) k -> p (j k)", j=ROWS_PP),
+                )
+            nc.sync.dma_start(
+                out=wp_rows[h][:].rearrange("p c j n -> p c (j n)"),
+                in_=W_proj[h].rearrange("(c p j) n -> p c (j n)", c=PASSES, p=P, j=PACK),
+            )
+
+        wo_rows = [keep.tile([P, PACK, DOUT], BF16, name="wo_rows%d" % g) for g in range(PASSES)]
+        wo_view = W_out.rearrange("(g t p) n -> g p t n", g=PASSES, t=PACK, p=P)
+        for g in range(PASSES):
+            nc.sync.dma_start(out=wo_rows[g][:], in_=wo_view[g])
+
+        warm = keep.tile([P, 1], F32)
+        nc.vector.memset(warm[:], 1.0)
+        nc.scalar.activation(out=warm[:], in_=warm[:], func=ACT.Sqrt)
         ident_f32 = keep.tile([P, P], F32)
         make_identity(nc, ident_f32[:])
         ones = keep.tile([P, P], BF16)
         nc.gpsimd.memset(ones[:], 1.0)
         ident_bf16 = keep.tile([P, P], BF16)
         make_identity(nc, ident_bf16[:])
-        exponent = keep.tile([P, H], F32)
-        nc.gpsimd.memset(exponent[:], 1.0 / DECAY_CONSTANT)
 
         x_words = x_sb[:].bitcast(F32).rearrange("r (c p u) -> r c u p", c=PASSES, p=P, u=2)
-        xT = psum.tile([P, PASSES, 2, B], F32)
+        xT = psum.tile([P, PASSES, 2, B], F32, tag="bank_left")
         for c in range(PASSES):
             for u in range(2):
                 nc.tensor.transpose(xT[:, c, u, :], x_words[:, c, u, :], ident_f32[:])
@@ -108,7 +112,7 @@ def tile_mixedrepeatheads_s_kernel(
             in_=x_grouped[:],
         )
 
-        bout_ps = psum.tile([P, DOUT], F32)
+        bout_ps = psum.tile([P, DOUT], F32, tag="bank_right")
         nc.tensor.matmul(bout_ps[:], lhsT=ones[:], rhs=bout_row[:], start=True, stop=True)
         bout_all = keep.tile([P, DOUT], F32)
         nc.scalar.copy(out=bout_all[:], in_=bout_ps[:])
@@ -120,13 +124,14 @@ def tile_mixedrepeatheads_s_kernel(
         w_all = small_all[:, W_AT : W_AT + H]
         b_all = small_all[:, B_AT : B_AT + H]
 
-        coef = keep.tile([P, H], F32)
-        nc.gpsimd.tensor_scalar(
-            out=coef[:], in0=small_all[:, DECAY_AT : DECAY_AT + H],
+        clipped = keep.tile([P, H], F32)
+        nc.vector.tensor_scalar(
+            out=clipped[:], in0=small_ps[:, DECAY_AT : DECAY_AT + H],
             scalar1=0.9, scalar2=1.0, op0=ALU.max, op1=ALU.min,
         )
-        nc.gpsimd.tensor_tensor(out=coef[:], in0=coef[:], in1=exponent[:], op=ALU.pow)
-        nc.gpsimd.tensor_tensor(out=coef[:, 0:H2], in0=coef[:, 0:H2], in1=w_all[:, 0:H2], op=ALU.mult)
+        coef = keep.tile([P, H], F32)
+        nc.scalar.activation(out=coef[:], in_=clipped[:], func=ACT.Sqrt)
+        nc.vector.tensor_tensor(out=coef[:, 0:H2], in0=coef[:, 0:H2], in1=w_all[:, 0:H2], op=ALU.mult)
 
         bprojT = psum.tile([P, P], BF16)
         nc.tensor.transpose(bprojT[:], bproj_rows[:], ident_bf16[:])
@@ -138,7 +143,7 @@ def tile_mixedrepeatheads_s_kernel(
         wp_codes = [keep.tile([P, PASSES, HID], U32, name="wp_codes%d" % h, align_bytes=64) for h in range(H)]
         wp_scales = [keep.tile([P, PASSES, HID], U8, name="wp_scales%d" % h, align_bytes=64) for h in range(H)]
         projT = [psum.tile([P, PACK, B], F32, name="projT%d" % g) for g in range(PASSES)]
-        cachesT = psum.tile([P, H, B], BF16)
+        cachesT = psum.tile([P, ROWS_PP, P], BF16)
         rest = keep.tile([P, H, B], F32)
         hid = [keep.tile([P, PACK, B], BF16, name="hid%d" % g) for g in range(PASSES)]
         hid_grouped = [keep.tile([P, B, PACK], BF16, name="hid_grouped%d" % g, align_bytes=64) for g in range(PASSES)]
@@ -168,12 +173,13 @@ def tile_mixedrepeatheads_s_kernel(
                     )
 
             if g == 0:
-                for h in range(H):
-                    nc.tensor.transpose(cachesT[:, h, :], caches_sb[:, h, :], ident_bf16[:])
+                for j in range(ROWS_PP):
+                    nc.tensor.transpose(cachesT[:, j, :], caches_sb[:, j, :], ident_bf16[:])
                 for h in range(H):
                     nc.scalar.activation(
-                        out=rest[:, h, :], in_=cachesT[:, h, :], func=ACT.Identity,
-                        scale=coef[:, h : h + 1], bias=shift[:, h : h + 1],
+                        out=rest[:, h, :].rearrange("k (q j) -> k q j", j=ROWS_PP),
+                        in_=cachesT[:, :, PARTS_PH * h : PARTS_PH * (h + 1)].rearrange("k j q -> k q j"),
+                        func=ACT.Identity, scale=coef[:, h : h + 1], bias=shift[:, h : h + 1],
                     )
 
             for t in range(PACK):
@@ -192,7 +198,10 @@ def tile_mixedrepeatheads_s_kernel(
         wo_grouped = [keep.tile([P, DOUT, PACK], BF16, name="wo_grouped%d" % g, align_bytes=64) for g in range(PASSES)]
         wo_codes = [keep.tile([P, DOUT], U32, name="wo_codes%d" % g, align_bytes=64) for g in range(PASSES)]
         wo_scales = [keep.tile([P, DOUT], U8, name="wo_scales%d" % g, align_bytes=64) for g in range(PASSES)]
-        acc = psum.tile([P, DOUT], F32)
+        acc = [
+            psum.tile([P, HALF], F32, name="acc_left", tag="bank_left"),
+            psum.tile([P, HALF], F32, name="acc_right", tag="bank_right"),
+        ]
         for g in range(PASSES):
             for half, copy in enumerate((nc.vector.tensor_copy, nc.scalar.copy)):
                 cols = slice(half * HALF, (half + 1) * HALF)
@@ -204,16 +213,18 @@ def tile_mixedrepeatheads_s_kernel(
                     scales=wo_scales[g][:, cols],
                     in_=wo_grouped[g][:, cols, :].rearrange("p n j -> p (n j)"),
                 )
-            nc.tensor.matmul_mx(
-                out=acc[:],
-                lhsT=hid_codes[g][:].bitcast(FP8X4),
-                lhsT_scale=hid_scales[g][:],
-                rhs=wo_codes[g][:].bitcast(FP8X4),
-                rhs_scale=wo_scales[g][:],
-                start=(g == 0),
-                stop=(g == PASSES - 1),
-            )
+                nc.tensor.matmul_mx(
+                    out=acc[half][:],
+                    lhsT=hid_codes[g][:].bitcast(FP8X4),
+                    lhsT_scale=hid_scales[g][:],
+                    rhs=wo_codes[g][:, cols].bitcast(FP8X4),
+                    rhs_scale=wo_scales[g][:, cols],
+                    start=(g == 0),
+                    stop=(g == PASSES - 1),
+                )
 
         result = keep.tile([P, DOUT], F32)
-        nc.vector.tensor_tensor(out=result[:], in0=acc[:], in1=bout_all[:], op=ALU.add)
-        nc.sync.dma_start(out=out, in_=result[:])
+        for half in range(2):
+            cols = slice(half * HALF, (half + 1) * HALF)
+            nc.vector.tensor_tensor(out=result[:, cols], in0=acc[half][:], in1=bout_all[:, cols], op=ALU.add)
+            nc.sync.dma_start(out=out[:, cols], in_=result[:, cols])

@@ -19,10 +19,14 @@ H2 = H // 2
 PASSES = DIM // K_PASS
 RUN = 4
 HALF = DOUT // 2
+LEFT, RIGHT = 0, 1
 ROWS_PP = H * B // P
 PARTS_PH = P // H
 
-W_AT, B_AT, DECAY_AT, SMALL = 0, 16, 32, 64
+PER_HEAD = 3
+COLUMN_STEP = 16
+SPREAD = 32
+W_AT, B_AT, DECAY_AT = 0, SPREAD, 2 * SPREAD
 
 FLOPS = 2 * B * DIM * H * HID + 2 * B * H * HID * DOUT
 
@@ -41,32 +45,126 @@ def tile_mixedrepeatheads_s_kernel(
     with ExitStack() as ctx:
         keep = ctx.enter_context(tc.tile_pool(name="keep", bufs=1))
         psum = ctx.enter_context(tc.psum_pool(name="psum", bufs=1))
+        ctx.enter_context(tc.manual_schedule())
 
         bout_row = keep.tile([P, DOUT], BF16)
-        small_row = keep.tile([P, SMALL], BF16)
+        per_head = keep.tile([P, PER_HEAD * COLUMN_STEP], BF16)
         bproj_rows = keep.tile([P, P], BF16)
-        nc.vector.memset(bout_row[:], 0.0)
-        nc.vector.memset(small_row[:], 0.0)
-        nc.vector.memset(bproj_rows[:], 0.0)
-        nc.scalar.dma_start(out=bout_row[0:1, :], in_=b_out.rearrange("(o n) -> o n", o=1))
-        nc.scalar.dma_start(out=bproj_rows[0:H, :], in_=b_proj)
-        nc.scalar.dma_start(
-            out=small_row[0:1, DECAY_AT : DECAY_AT + H],
-            in_=decay_values.rearrange("(o h) -> o h", o=1),
-        )
-        with nc.allow_non_contiguous_dma(reason="column index of w_mix and b_mix: 8 elements each"):
-            nc.scalar.dma_start(
-                out=small_row[0:1, W_AT : W_AT + H],
-                in_=w_mix[:, index : index + 1].rearrange("h o -> o h"),
-            )
-            nc.scalar.dma_start(
-                out=small_row[0:1, B_AT : B_AT + H],
-                in_=b_mix[:, index : index + 1].rearrange("h o -> o h"),
-            )
-
         x_sb = keep.tile([P, DIM], BF16)
         wp_rows = [keep.tile([P, PASSES, PACK, HID], BF16, name="wp_rows%d" % h) for h in range(H)]
         caches_sb = keep.tile([P, ROWS_PP, HID], BF16)
+        wo_rows = [keep.tile([P, PACK, DOUT], BF16, name="wo_rows%d" % g) for g in range(PASSES)]
+
+        x_grouped = keep.tile([P, PASSES * B * PACK], BF16, align_bytes=64)
+        x_codes = keep.tile([P, PASSES, B], U32, align_bytes=64)
+        x_scales = keep.tile([P, PASSES, B], U8, align_bytes=64)
+        wp_grouped = [keep.tile([P, PASSES, HID, PACK], BF16, name="wp_grouped%d" % h, align_bytes=64) for h in range(H)]
+        wp_codes = [keep.tile([P, PASSES, HID], U32, name="wp_codes%d" % h, align_bytes=64) for h in range(H)]
+        wp_scales = [keep.tile([P, PASSES, HID], U8, name="wp_scales%d" % h, align_bytes=64) for h in range(H)]
+        rest = keep.tile([P, H, B], F32)
+        hid = [keep.tile([P, PACK, B], BF16, name="hid%d" % g) for g in range(PASSES)]
+        hid_grouped = [keep.tile([P, B, PACK], BF16, name="hid_grouped%d" % g, align_bytes=64) for g in range(PASSES)]
+        hid_codes = [keep.tile([P, B], U32, name="hid_codes%d" % g, align_bytes=64) for g in range(PASSES)]
+        hid_scales = [keep.tile([P, B], U8, name="hid_scales%d" % g, align_bytes=64) for g in range(PASSES)]
+        wo_grouped = [keep.tile([P, DOUT, PACK], BF16, name="wo_grouped%d" % g, align_bytes=64) for g in range(PASSES)]
+        wo_codes = [keep.tile([P, DOUT], U32, name="wo_codes%d" % g, align_bytes=64) for g in range(PASSES)]
+        wo_scales = [keep.tile([P, DOUT], U8, name="wo_scales%d" % g, align_bytes=64) for g in range(PASSES)]
+        result = keep.tile([P, DOUT], F32)
+
+        xT = psum.tile([P, PASSES, 2, B], F32, tag="bank_left")
+        bout_ps = psum.tile([P, DOUT], F32, tag="bank_right")
+        small_ps = psum.tile([P, PER_HEAD * SPREAD], F32)
+        bprojT = psum.tile([P, P], BF16)
+        cachesT = psum.tile([P, ROWS_PP, P], BF16)
+        projT = [psum.tile([P, PACK, B], F32, name="projT%d" % g) for g in range(PASSES)]
+
+        def regroup_head(h):
+            copy = nc.vector.tensor_copy if h % 2 == 0 else nc.scalar.copy
+            for c in range(PASSES):
+                regroup(copy, wp_grouped[h][:, c], wp_rows[h][:, c])
+
+        def quantise_head(h):
+            nc.vector.quantize_mx(
+                out=wp_codes[h][:].rearrange("p c n -> p (c n)").bitcast(FP8X4),
+                scales=wp_scales[h][:].rearrange("p c n -> p (c n)"),
+                in_=wp_grouped[h][:].rearrange("p c n j -> p (c n j)"),
+            )
+
+        def project_head(h):
+            for c in range(PASSES):
+                nc.tensor.matmul_mx(
+                    out=projT[h // PACK][:, h % PACK, :],
+                    lhsT=wp_codes[h][:, c, :].bitcast(FP8X4),
+                    lhsT_scale=wp_scales[h][:, c, :],
+                    rhs=x_codes[:, c, :].bitcast(FP8X4),
+                    rhs_scale=x_scales[:, c, :],
+                    start=(c == 0),
+                    stop=(c == PASSES - 1),
+                )
+
+        def prepare_rest(g):
+            for h in range(PACK * g, PACK * (g + 1)):
+                nc.scalar.activation(
+                    out=rest[:, h, :].rearrange("k (q j) -> k q j", j=ROWS_PP),
+                    in_=cachesT[:, :, PARTS_PH * h : PARTS_PH * (h + 1)].rearrange("k j q -> k q j"),
+                    func=ACT.Identity, scale=coef[:, h : h + 1], bias=shift[:, h : h + 1],
+                )
+
+        def mix(g):
+            for t in range(PACK):
+                h = PACK * g + t
+                nc.vector.scalar_tensor_tensor(
+                    out=hid[g][:, t, :], in0=projT[g][:, t, :], scalar=w_all[:, h : h + 1],
+                    in1=rest[:, h, :], op0=ALU.mult, op1=ALU.add,
+                )
+
+        def quantise_hidden(g):
+            nc.vector.quantize_mx(
+                out=hid_codes[g][:].bitcast(FP8X4),
+                scales=hid_scales[g][:],
+                in_=hid_grouped[g][:].rearrange("p r t -> p (r t)"),
+            )
+
+        def regroup_w_out(g):
+            for half, copy in ((LEFT, nc.vector.tensor_copy), (RIGHT, nc.scalar.copy)):
+                cols = slice(half * HALF, (half + 1) * HALF)
+                regroup(copy, wo_grouped[g][:, cols, :], wo_rows[g][:, :, cols])
+
+        def quantise_w_out(g, half):
+            cols = slice(half * HALF, (half + 1) * HALF)
+            nc.vector.quantize_mx(
+                out=wo_codes[g][:, cols].bitcast(FP8X4),
+                scales=wo_scales[g][:, cols],
+                in_=wo_grouped[g][:, cols, :].rearrange("p n j -> p (n j)"),
+            )
+
+        def multiply(g, half):
+            cols = slice(half * HALF, (half + 1) * HALF)
+            nc.tensor.matmul_mx(
+                out=acc[half][:],
+                lhsT=hid_codes[g][:].bitcast(FP8X4),
+                lhsT_scale=hid_scales[g][:],
+                rhs=wo_codes[g][:, cols].bitcast(FP8X4),
+                rhs_scale=wo_scales[g][:, cols],
+                start=(g == 0),
+                stop=(g == PASSES - 1),
+            )
+
+        nc.vector.memset(per_head[:], 0.0)
+        nc.vector.memset(bproj_rows[:], 0.0)
+        nc.vector.memset(bout_row[:], 0.0)
+        per_head_sources = (
+            w_mix[:, index : index + 1],
+            b_mix[:, index : index + 1],
+            decay_values.rearrange("(h o) -> h o", o=1),
+        )
+        for i in range(PER_HEAD):
+            nc.scalar.dma_start(
+                out=per_head[0:H, COLUMN_STEP * i : COLUMN_STEP * i + 1], in_=per_head_sources[i]
+            )
+        nc.scalar.dma_start(out=bproj_rows[0:H, :], in_=b_proj)
+        nc.scalar.dma_start(out=bout_row[0:1, :], in_=b_out.rearrange("(o n) -> o n", o=1))
+
         for h in range(H):
             if h == 2:
                 nc.sync.dma_start(out=x_sb[:], in_=x)
@@ -78,8 +176,6 @@ def tile_mixedrepeatheads_s_kernel(
                 out=wp_rows[h][:].rearrange("p c j n -> p c (j n)"),
                 in_=W_proj[h].rearrange("(c p j) n -> p c (j n)", c=PASSES, p=P, j=PACK),
             )
-
-        wo_rows = [keep.tile([P, PACK, DOUT], BF16, name="wo_rows%d" % g) for g in range(PASSES)]
         wo_view = W_out.rearrange("(g t p) n -> g p t n", g=PASSES, t=PACK, p=P)
         for g in range(PASSES):
             nc.sync.dma_start(out=wo_rows[g][:], in_=wo_view[g])
@@ -87,42 +183,26 @@ def tile_mixedrepeatheads_s_kernel(
         warm = keep.tile([P, 1], F32)
         nc.vector.memset(warm[:], 1.0)
         nc.scalar.activation(out=warm[:], in_=warm[:], func=ACT.Sqrt)
-        ident_f32 = keep.tile([P, P], F32)
-        make_identity(nc, ident_f32[:])
         ones = keep.tile([P, P], BF16)
         nc.gpsimd.memset(ones[:], 1.0)
         ident_bf16 = keep.tile([P, P], BF16)
         make_identity(nc, ident_bf16[:])
+        ident_f32 = keep.tile([P, P], F32)
+        make_identity(nc, ident_f32[:])
 
-        x_words = x_sb[:].bitcast(F32).rearrange("r (c p u) -> r c u p", c=PASSES, p=P, u=2)
-        xT = psum.tile([P, PASSES, 2, B], F32, tag="bank_left")
-        for c in range(PASSES):
-            for u in range(2):
-                nc.tensor.transpose(xT[:, c, u, :], x_words[:, c, u, :], ident_f32[:])
-        x_grouped = keep.tile([P, PASSES * B * PACK], BF16, align_bytes=64)
-        nc.scalar.copy(
-            out=x_grouped[:].bitcast(F32).rearrange("p (c r u) -> p c r u", c=PASSES, r=B, u=2),
-            in_=xT[:].rearrange("p c u r -> p c r u"),
-        )
-        x_codes = keep.tile([P, PASSES, B], U32, align_bytes=64)
-        x_scales = keep.tile([P, PASSES, B], U8, align_bytes=64)
-        nc.vector.quantize_mx(
-            out=x_codes[:].rearrange("p c r -> p (c r)").bitcast(FP8X4),
-            scales=x_scales[:].rearrange("p c r -> p (c r)"),
-            in_=x_grouped[:],
-        )
+        regroup_head(0)
+        regroup_head(1)
 
-        bout_ps = psum.tile([P, DOUT], F32, tag="bank_right")
+        for i in range(PER_HEAD):
+            nc.tensor.matmul(
+                small_ps[:, SPREAD * i : SPREAD * (i + 1)],
+                lhsT=per_head[:, COLUMN_STEP * i : COLUMN_STEP * i + 1].to_broadcast([P, P]),
+                rhs=ident_bf16[:, 0:SPREAD],
+                start=True,
+                stop=True,
+            )
+        nc.tensor.transpose(bprojT[:], bproj_rows[:], ident_bf16[:])
         nc.tensor.matmul(bout_ps[:], lhsT=ones[:], rhs=bout_row[:], start=True, stop=True)
-        bout_all = keep.tile([P, DOUT], F32)
-        nc.scalar.copy(out=bout_all[:], in_=bout_ps[:])
-
-        small_ps = psum.tile([P, SMALL], F32)
-        nc.tensor.matmul(small_ps[:], lhsT=ones[:], rhs=small_row[:], start=True, stop=True)
-        small_all = keep.tile([P, SMALL], F32)
-        nc.vector.tensor_copy(out=small_all[:], in_=small_ps[:])
-        w_all = small_all[:, W_AT : W_AT + H]
-        b_all = small_all[:, B_AT : B_AT + H]
 
         clipped = keep.tile([P, H], F32)
         nc.vector.tensor_scalar(
@@ -131,100 +211,72 @@ def tile_mixedrepeatheads_s_kernel(
         )
         coef = keep.tile([P, H], F32)
         nc.scalar.activation(out=coef[:], in_=clipped[:], func=ACT.Sqrt)
-        nc.vector.tensor_tensor(out=coef[:, 0:H2], in0=coef[:, 0:H2], in1=w_all[:, 0:H2], op=ALU.mult)
-
-        bprojT = psum.tile([P, P], BF16)
-        nc.tensor.transpose(bprojT[:], bproj_rows[:], ident_bf16[:])
+        small_all = keep.tile([P, PER_HEAD * SPREAD], F32)
+        nc.vector.tensor_copy(out=small_all[:], in_=small_ps[:])
+        w_all = small_all[:, W_AT : W_AT + H]
+        b_all = small_all[:, B_AT : B_AT + H]
+        quantise_head(0)
+        bout_all = keep.tile([P, DOUT], F32)
+        nc.vector.tensor_copy(out=bout_all[:], in_=bout_ps[:])
         shift = keep.tile([P, H], F32)
         nc.vector.tensor_tensor(out=shift[:], in0=bprojT[:, 0:H], in1=w_all, op=ALU.mult)
+        nc.vector.tensor_tensor(out=coef[:, 0:H2], in0=coef[:, 0:H2], in1=w_all[:, 0:H2], op=ALU.mult)
         nc.vector.tensor_tensor(out=shift[:], in0=shift[:], in1=b_all, op=ALU.add)
 
-        wp_grouped = [keep.tile([P, PASSES, HID, PACK], BF16, name="wp_grouped%d" % h, align_bytes=64) for h in range(H)]
-        wp_codes = [keep.tile([P, PASSES, HID], U32, name="wp_codes%d" % h, align_bytes=64) for h in range(H)]
-        wp_scales = [keep.tile([P, PASSES, HID], U8, name="wp_scales%d" % h, align_bytes=64) for h in range(H)]
-        projT = [psum.tile([P, PACK, B], F32, name="projT%d" % g) for g in range(PASSES)]
-        cachesT = psum.tile([P, ROWS_PP, P], BF16)
-        rest = keep.tile([P, H, B], F32)
-        hid = [keep.tile([P, PACK, B], BF16, name="hid%d" % g) for g in range(PASSES)]
-        hid_grouped = [keep.tile([P, B, PACK], BF16, name="hid_grouped%d" % g, align_bytes=64) for g in range(PASSES)]
-        hid_codes = [keep.tile([P, B], U32, name="hid_codes%d" % g, align_bytes=64) for g in range(PASSES)]
-        hid_scales = [keep.tile([P, B], U8, name="hid_scales%d" % g, align_bytes=64) for g in range(PASSES)]
+        x_words = x_sb[:].bitcast(F32).rearrange("r (c p u) -> r c u p", c=PASSES, p=P, u=2)
+        for c in range(PASSES):
+            for u in range(2):
+                nc.tensor.transpose(xT[:, c, u, :], x_words[:, c, u, :], ident_f32[:])
+        nc.scalar.copy(
+            out=x_grouped[:].bitcast(F32).rearrange("p (c r u) -> p c r u", c=PASSES, r=B, u=2),
+            in_=xT[:].rearrange("p c u r -> p c r u"),
+        )
+        for j in range(ROWS_PP):
+            nc.tensor.transpose(cachesT[:, j, :], caches_sb[:, j, :], ident_bf16[:])
 
+        regroup_head(2)
+        regroup_head(3)
+        quantise_head(1)
+        nc.vector.quantize_mx(
+            out=x_codes[:].rearrange("p c r -> p (c r)").bitcast(FP8X4),
+            scales=x_scales[:].rearrange("p c r -> p (c r)"),
+            in_=x_grouped[:],
+        )
+        quantise_head(2)
+        for h in range(3):
+            project_head(h)
         for g in range(PASSES):
-            for t in range(PACK):
-                h = PACK * g + t
-                copy = nc.vector.tensor_copy if h % 2 == 0 else nc.scalar.copy
-                for c in range(PASSES):
-                    regroup(copy, wp_grouped[h][:, c], wp_rows[h][:, c])
-                nc.vector.quantize_mx(
-                    out=wp_codes[h][:].rearrange("p c n -> p (c n)").bitcast(FP8X4),
-                    scales=wp_scales[h][:].rearrange("p c n -> p (c n)"),
-                    in_=wp_grouped[h][:].rearrange("p c n j -> p (c n j)"),
-                )
-                for c in range(PASSES):
-                    nc.tensor.matmul_mx(
-                        out=projT[g][:, t, :],
-                        lhsT=wp_codes[h][:, c, :].bitcast(FP8X4),
-                        lhsT_scale=wp_scales[h][:, c, :],
-                        rhs=x_codes[:, c, :].bitcast(FP8X4),
-                        rhs_scale=x_scales[:, c, :],
-                        start=(c == 0),
-                        stop=(c == PASSES - 1),
-                    )
+            regroup_head(4 + 2 * g)
+            regroup_head(5 + 2 * g)
+            prepare_rest(g)
+            for h in (3 + 2 * g, 4 + 2 * g):
+                quantise_head(h)
+                project_head(h)
 
-            if g == 0:
-                for j in range(ROWS_PP):
-                    nc.tensor.transpose(cachesT[:, j, :], caches_sb[:, j, :], ident_bf16[:])
-                for h in range(H):
-                    nc.scalar.activation(
-                        out=rest[:, h, :].rearrange("k (q j) -> k q j", j=ROWS_PP),
-                        in_=cachesT[:, :, PARTS_PH * h : PARTS_PH * (h + 1)].rearrange("k j q -> k q j"),
-                        func=ACT.Identity, scale=coef[:, h : h + 1], bias=shift[:, h : h + 1],
-                    )
-
-            for t in range(PACK):
-                h = PACK * g + t
-                nc.vector.scalar_tensor_tensor(
-                    out=hid[g][:, t, :], in0=projT[g][:, t, :], scalar=w_all[:, h : h + 1],
-                    in1=rest[:, h, :], op0=ALU.mult, op1=ALU.add,
-                )
-            regroup(nc.vector.tensor_copy, hid_grouped[g][:], hid[g][:])
-            nc.vector.quantize_mx(
-                out=hid_codes[g][:].bitcast(FP8X4),
-                scales=hid_scales[g][:],
-                in_=hid_grouped[g][:].rearrange("p r t -> p (r t)"),
-            )
-
-        wo_grouped = [keep.tile([P, DOUT, PACK], BF16, name="wo_grouped%d" % g, align_bytes=64) for g in range(PASSES)]
-        wo_codes = [keep.tile([P, DOUT], U32, name="wo_codes%d" % g, align_bytes=64) for g in range(PASSES)]
-        wo_scales = [keep.tile([P, DOUT], U8, name="wo_scales%d" % g, align_bytes=64) for g in range(PASSES)]
         acc = [
             psum.tile([P, HALF], F32, name="acc_left", tag="bank_left"),
             psum.tile([P, HALF], F32, name="acc_right", tag="bank_right"),
         ]
-        for g in range(PASSES):
-            for half, copy in enumerate((nc.vector.tensor_copy, nc.scalar.copy)):
-                cols = slice(half * HALF, (half + 1) * HALF)
-                regroup(copy, wo_grouped[g][:, cols, :], wo_rows[g][:, :, cols])
-            for half in range(2):
-                cols = slice(half * HALF, (half + 1) * HALF)
-                nc.vector.quantize_mx(
-                    out=wo_codes[g][:, cols].bitcast(FP8X4),
-                    scales=wo_scales[g][:, cols],
-                    in_=wo_grouped[g][:, cols, :].rearrange("p n j -> p (n j)"),
-                )
-                nc.tensor.matmul_mx(
-                    out=acc[half][:],
-                    lhsT=hid_codes[g][:].bitcast(FP8X4),
-                    lhsT_scale=hid_scales[g][:],
-                    rhs=wo_codes[g][:, cols].bitcast(FP8X4),
-                    rhs_scale=wo_scales[g][:, cols],
-                    start=(g == 0),
-                    stop=(g == PASSES - 1),
-                )
+        mix(0)
+        regroup_w_out(0)
+        quantise_head(7)
+        project_head(7)
+        regroup(nc.vector.tensor_copy, hid_grouped[0][:], hid[0][:])
+        quantise_w_out(0, LEFT)
+        quantise_hidden(0)
+        multiply(0, LEFT)
+        regroup_w_out(1)
+        mix(1)
+        quantise_w_out(0, RIGHT)
+        multiply(0, RIGHT)
+        regroup(nc.vector.tensor_copy, hid_grouped[1][:], hid[1][:])
+        quantise_w_out(1, LEFT)
+        quantise_hidden(1)
+        multiply(1, LEFT)
+        quantise_w_out(1, RIGHT)
+        multiply(1, RIGHT)
 
-        result = keep.tile([P, DOUT], F32)
-        for half in range(2):
+        for half in (LEFT, RIGHT):
             cols = slice(half * HALF, (half + 1) * HALF)
             nc.vector.tensor_tensor(out=result[:, cols], in0=acc[half][:], in1=bout_all[:, cols], op=ALU.add)
             nc.sync.dma_start(out=out[:, cols], in_=result[:, cols])

@@ -79,9 +79,14 @@ def tile_mixedrepeatheads_s_kernel(
         projT = [psum.tile([P, PACK, B], F32, name="projT%d" % g) for g in range(PASSES)]
 
         def regroup_head(h):
-            copy = nc.vector.tensor_copy if h % 2 == 0 else nc.scalar.copy
-            for c in range(PASSES):
-                regroup(copy, wp_grouped[h][:, c], wp_rows[h][:, c])
+            if h % 2 == 0:
+                nc.vector.tensor_copy(
+                    out=wp_grouped[h][:].rearrange("p c (a i) j -> p c a j i", i=RUN),
+                    in_=wp_rows[h][:].rearrange("p c j (a i) -> p c a j i", i=RUN),
+                )
+            else:
+                for c in range(PASSES):
+                    regroup(nc.scalar.copy, wp_grouped[h][:, c], wp_rows[h][:, c])
 
         def quantise_head(h):
             nc.vector.quantize_mx(

@@ -15,27 +15,18 @@ P = 128
 PACK = 4
 K_PASS = P * PACK
 B, DIM, HID, H, DOUT = 128, 1024, 128, 8, 512
-H2 = H // 2
 PASSES = DIM // K_PASS
+HEADS_PG = H // PASSES
+Q = HID // PACK
 RUN = 4
 HALF = DOUT // 2
 LEFT, RIGHT = 0, 1
-ROWS_PP = H * B // P
-PARTS_PH = P // H
 
 PER_HEAD = 3
 COLUMN_STEP = 16
-SPREAD = 32
-W_AT, B_AT, DECAY_AT = 0, SPREAD, 2 * SPREAD
+W_AT, B_AT, DECAY_AT = 0, 1, 2
 
 FLOPS = 2 * B * DIM * H * HID + 2 * B * H * HID * DOUT
-
-
-def regroup(copy, grouped, rows):
-    copy(
-        out=grouped.rearrange("p (a i) j -> p a j i", i=RUN),
-        in_=rows.rearrange("p j (a i) -> p a j i", i=RUN),
-    )
 
 
 def tile_mixedrepeatheads_s_kernel(
@@ -47,22 +38,24 @@ def tile_mixedrepeatheads_s_kernel(
         psum = ctx.enter_context(tc.psum_pool(name="psum", bufs=1))
         ctx.enter_context(tc.manual_schedule())
 
-        bout_row = keep.tile([P, DOUT], BF16)
+        bout_all = keep.tile([P, DOUT], BF16)
         per_head = keep.tile([P, PER_HEAD * COLUMN_STEP], BF16)
-        bproj_rows = keep.tile([P, P], BF16)
+        bproj = keep.tile([P, PASSES, COLUMN_STEP], BF16)
         x_sb = keep.tile([P, DIM], BF16)
         wp_rows = [keep.tile([P, PASSES, PACK, HID], BF16, name="wp_rows%d" % h) for h in range(H)]
-        caches_sb = keep.tile([P, ROWS_PP, HID], BF16)
+        caches_sb = keep.tile([P, H, HID], BF16)
         wo_rows = [keep.tile([P, PACK, DOUT], BF16, name="wo_rows%d" % g) for g in range(PASSES)]
 
         x_grouped = keep.tile([P, PASSES * B * PACK], BF16, align_bytes=64)
         x_codes = keep.tile([P, PASSES, B], U32, align_bytes=64)
         x_scales = keep.tile([P, PASSES, B], U8, align_bytes=64)
-        wp_grouped = [keep.tile([P, PASSES, HID, PACK], BF16, name="wp_grouped%d" % h, align_bytes=64) for h in range(H)]
-        wp_codes = [keep.tile([P, PASSES, HID], U32, name="wp_codes%d" % h, align_bytes=64) for h in range(H)]
-        wp_scales = [keep.tile([P, PASSES, HID], U8, name="wp_scales%d" % h, align_bytes=64) for h in range(H)]
-        rest = keep.tile([P, H, B], F32)
-        hid = [keep.tile([P, PACK, B], BF16, name="hid%d" % g) for g in range(PASSES)]
+        wp_grouped = [
+            keep.tile([P, PACK, PASSES, HEADS_PG, Q, PACK], BF16, name="wp_grouped%d" % g, align_bytes=64)
+            for g in range(PASSES)
+        ]
+        wp_codes = [keep.tile([P, PACK, PASSES, P], U32, name="wp_codes%d" % g, align_bytes=64) for g in range(PASSES)]
+        wp_scales = [keep.tile([P, PACK, PASSES, P], U8, name="wp_scales%d" % g, align_bytes=64) for g in range(PASSES)]
+        rest = [keep.tile([P, PACK, B], F32, name="rest%d" % g) for g in range(PASSES)]
         hid_grouped = [keep.tile([P, B, PACK], BF16, name="hid_grouped%d" % g, align_bytes=64) for g in range(PASSES)]
         hid_codes = [keep.tile([P, B], U32, name="hid_codes%d" % g, align_bytes=64) for g in range(PASSES)]
         hid_scales = [keep.tile([P, B], U8, name="hid_scales%d" % g, align_bytes=64) for g in range(PASSES)]
@@ -71,57 +64,54 @@ def tile_mixedrepeatheads_s_kernel(
         wo_scales = [keep.tile([P, DOUT], U8, name="wo_scales%d" % g, align_bytes=64) for g in range(PASSES)]
         result = keep.tile([P, DOUT], F32)
 
-        xT = psum.tile([P, PASSES, 2, B], F32, tag="bank_left")
-        bout_ps = psum.tile([P, DOUT], F32, tag="bank_right")
-        small_ps = psum.tile([P, PER_HEAD * SPREAD], F32)
-        bprojT = psum.tile([P, P], BF16)
-        cachesT = psum.tile([P, ROWS_PP, P], BF16)
+        xT = psum.tile([P, PASSES, 2, B], F32)
+        cachesT = psum.tile([P, PASSES, 2, B], F32)
+        small_ps = psum.tile([P, PASSES, PACK], F32)
         projT = [psum.tile([P, PACK, B], F32, name="projT%d" % g) for g in range(PASSES)]
+        acc = [psum.tile([P, HALF], F32, name="acc%d" % half) for half in (LEFT, RIGHT)]
 
-        def regroup_head(h):
-            if h % 2 == 0:
-                nc.vector.tensor_copy(
-                    out=wp_grouped[h][:].rearrange("p c (a i) j -> p c a j i", i=RUN),
-                    in_=wp_rows[h][:].rearrange("p c j (a i) -> p c a j i", i=RUN),
-                )
-            else:
-                for c in range(PASSES):
-                    regroup(nc.scalar.copy, wp_grouped[h][:, c], wp_rows[h][:, c])
-
-        def quantise_head(h):
-            nc.vector.quantize_mx(
-                out=wp_codes[h][:].rearrange("p c n -> p (c n)").bitcast(FP8X4),
-                scales=wp_scales[h][:].rearrange("p c n -> p (c n)"),
-                in_=wp_grouped[h][:].rearrange("p c n j -> p (c n j)"),
+        def regroup_head(copy, h, c):
+            g, i = divmod(h, HEADS_PG)
+            copy(
+                out=wp_grouped[g][:, :, c, i, :, :].rearrange("p t q j -> p q j t"),
+                in_=wp_rows[h][:, c, :, :].rearrange("p j (q t) -> p q j t", t=PACK),
             )
 
-        def project_head(h):
-            for c in range(PASSES):
-                nc.tensor.matmul_mx(
-                    out=projT[h // PACK][:, h % PACK, :],
-                    lhsT=wp_codes[h][:, c, :].bitcast(FP8X4),
-                    lhsT_scale=wp_scales[h][:, c, :],
-                    rhs=x_codes[:, c, :].bitcast(FP8X4),
-                    rhs_scale=x_scales[:, c, :],
-                    start=(c == 0),
-                    stop=(c == PASSES - 1),
-                )
+        def quantise_group(g, t0, t1):
+            nc.vector.quantize_mx(
+                out=wp_codes[g][:, t0:t1].rearrange("p t c m -> p (t c m)").bitcast(FP8X4),
+                scales=wp_scales[g][:, t0:t1].rearrange("p t c m -> p (t c m)"),
+                in_=wp_grouped[g][:, t0:t1].rearrange("p t c i q j -> p (t c i q j)"),
+            )
+
+        def project(g, t0, t1):
+            for t in range(t0, t1):
+                for c in range(PASSES):
+                    nc.tensor.matmul_mx(
+                        out=projT[g][:, t, :],
+                        lhsT=wp_codes[g][:, t, c, :].bitcast(FP8X4),
+                        lhsT_scale=wp_scales[g][:, t, c, :],
+                        rhs=x_codes[:, c, :].bitcast(FP8X4),
+                        rhs_scale=x_scales[:, c, :],
+                        start=(c == 0),
+                        stop=(c == PASSES - 1),
+                    )
 
         def prepare_rest(g):
-            for h in range(PACK * g, PACK * (g + 1)):
-                nc.scalar.activation(
-                    out=rest[:, h, :].rearrange("k (q j) -> k q j", j=ROWS_PP),
-                    in_=cachesT[:, :, PARTS_PH * h : PARTS_PH * (h + 1)].rearrange("k j q -> k q j"),
-                    func=ACT.Identity, scale=coef[:, h : h + 1], bias=shift[:, h : h + 1],
-                )
+            for u in range(2):
+                pair = cachesT[:, g, u, :].bitcast(BF16).rearrange("p (r e) -> p e r", e=2)
+                for e in range(2):
+                    t = 2 * u + e
+                    nc.scalar.activation(
+                        out=rest[g][:, t, :], in_=pair[:, e, :],
+                        func=ACT.Identity, scale=coef[:, g : g + 1], bias=shift[:, g, t : t + 1],
+                    )
 
         def mix(g):
-            for t in range(PACK):
-                h = PACK * g + t
-                nc.vector.scalar_tensor_tensor(
-                    out=hid[g][:, t, :], in0=projT[g][:, t, :], scalar=w_all[:, h : h + 1],
-                    in1=rest[:, h, :], op0=ALU.mult, op1=ALU.add,
-                )
+            nc.vector.scalar_tensor_tensor(
+                out=hid_grouped[g][:], in0=projT[g][:].rearrange("p t r -> p r t"), scalar=small[:, g, W_AT : W_AT + 1],
+                in1=rest[g][:].rearrange("p t r -> p r t"), op0=ALU.mult, op1=ALU.add,
+            )
 
         def quantise_hidden(g):
             nc.vector.quantize_mx(
@@ -130,13 +120,14 @@ def tile_mixedrepeatheads_s_kernel(
                 in_=hid_grouped[g][:].rearrange("p r t -> p (r t)"),
             )
 
-        def regroup_w_out(g):
-            for half, copy in ((LEFT, nc.vector.tensor_copy), (RIGHT, nc.scalar.copy)):
-                cols = slice(half * HALF, (half + 1) * HALF)
-                regroup(copy, wo_grouped[g][:, cols, :], wo_rows[g][:, :, cols])
+        def regroup_w_out(copy, g, c0, c1):
+            copy(
+                out=wo_grouped[g][:, c0:c1, :].rearrange("p (a i) j -> p a j i", i=RUN),
+                in_=wo_rows[g][:, :, c0:c1].rearrange("p j (a i) -> p a j i", i=RUN),
+            )
 
-        def quantise_w_out(g, half):
-            cols = slice(half * HALF, (half + 1) * HALF)
+        def quantise_w_out(g, c0, c1):
+            cols = slice(c0, c1)
             nc.vector.quantize_mx(
                 out=wo_codes[g][:, cols].bitcast(FP8X4),
                 scales=wo_scales[g][:, cols],
@@ -155,9 +146,12 @@ def tile_mixedrepeatheads_s_kernel(
                 stop=(g == PASSES - 1),
             )
 
-        nc.vector.memset(per_head[:], 0.0)
-        nc.vector.memset(bproj_rows[:], 0.0)
-        nc.vector.memset(bout_row[:], 0.0)
+        def finish(half):
+            cols = slice(half * HALF, (half + 1) * HALF)
+            nc.vector.tensor_tensor(out=result[:, cols], in0=acc[half][:], in1=bout_all[:, cols], op=ALU.add)
+            nc.sync.dma_start(out=out[:, cols], in_=result[:, cols])
+
+        nc.gpsimd.memset(per_head[:], 0.0)
         per_head_sources = (
             w_mix[:, index : index + 1],
             b_mix[:, index : index + 1],
@@ -167,121 +161,119 @@ def tile_mixedrepeatheads_s_kernel(
             nc.scalar.dma_start(
                 out=per_head[0:H, COLUMN_STEP * i : COLUMN_STEP * i + 1], in_=per_head_sources[i]
             )
-        nc.scalar.dma_start(out=bproj_rows[0:H, :], in_=b_proj)
-        nc.scalar.dma_start(out=bout_row[0:1, :], in_=b_out.rearrange("(o n) -> o n", o=1))
 
-        for h in range(H):
-            if h == 2:
-                nc.sync.dma_start(out=x_sb[:], in_=x)
-                nc.sync.dma_start(
-                    out=caches_sb[:].rearrange("p j k -> p (j k)"),
-                    in_=caches.rearrange("h r k -> (h r) k").rearrange("(p j) k -> p (j k)", j=ROWS_PP),
-                )
+        def load_head(h, c0=0, c1=PASSES):
             nc.sync.dma_start(
-                out=wp_rows[h][:].rearrange("p c j n -> p c (j n)"),
-                in_=W_proj[h].rearrange("(c p j) n -> p c (j n)", c=PASSES, p=P, j=PACK),
+                out=wp_rows[h][:, c0:c1].rearrange("p c j n -> p c (j n)"),
+                in_=W_proj[h].rearrange("(c p j) n -> p c (j n)", c=PASSES, p=P, j=PACK)[:, c0:c1, :],
             )
-        wo_view = W_out.rearrange("(g t p) n -> g p t n", g=PASSES, t=PACK, p=P)
+
+        load_head(0, 0, 1)
+        load_head(0, 1, 2)
+        load_head(1)
+        load_head(2)
+        nc.sync.dma_start(out=x_sb[:], in_=x)
+        for h in range(3, H):
+            load_head(h)
+        nc.sync.dma_start(out=caches_sb[:], in_=caches.rearrange("h r k -> r h k"))
+        wo_view = W_out.rearrange("(g p j) n -> g p (j n)", g=PASSES, p=P, j=PACK)
         for g in range(PASSES):
-            nc.sync.dma_start(out=wo_rows[g][:], in_=wo_view[g])
+            nc.sync.dma_start(out=wo_rows[g][:].rearrange("p j n -> p (j n)"), in_=wo_view[g])
 
         warm = keep.tile([P, 1], F32)
         nc.vector.memset(warm[:], 1.0)
         nc.scalar.activation(out=warm[:], in_=warm[:], func=ACT.Sqrt)
-        ones = keep.tile([P, P], BF16)
-        nc.gpsimd.memset(ones[:], 1.0)
-        ident_bf16 = keep.tile([P, P], BF16)
-        make_identity(nc, ident_bf16[:])
-        ident_f32 = keep.tile([P, P], F32)
-        make_identity(nc, ident_f32[:])
-
-        regroup_head(0)
-        regroup_head(1)
-
-        for i in range(PER_HEAD):
-            nc.tensor.matmul(
-                small_ps[:, SPREAD * i : SPREAD * (i + 1)],
-                lhsT=per_head[:, COLUMN_STEP * i : COLUMN_STEP * i + 1].to_broadcast([P, P]),
-                rhs=ident_bf16[:, 0:SPREAD],
-                start=True,
-                stop=True,
-            )
-        nc.tensor.transpose(bprojT[:], bproj_rows[:], ident_bf16[:])
-        nc.tensor.matmul(bout_ps[:], lhsT=ones[:], rhs=bout_row[:], start=True, stop=True)
-
-        clipped = keep.tile([P, H], F32)
-        nc.vector.tensor_scalar(
-            out=clipped[:], in0=small_ps[:, DECAY_AT : DECAY_AT + H],
-            scalar1=0.9, scalar2=1.0, op0=ALU.max, op1=ALU.min,
+        select = keep.tile([P, H, Q], BF16)
+        nc.gpsimd.memset(select[:], 0.0)
+        nc.gpsimd.affine_select(
+            out=select[:], in_=select[:], compare_op=ALU.not_equal, fill=1.0,
+            base=0, pattern=[[-1, H], [0, Q]], channel_multiplier=1,
         )
-        coef = keep.tile([P, H], F32)
-        nc.scalar.activation(out=coef[:], in_=clipped[:], func=ACT.Sqrt)
-        small_all = keep.tile([P, PER_HEAD * SPREAD], F32)
-        nc.vector.tensor_copy(out=small_all[:], in_=small_ps[:])
-        w_all = small_all[:, W_AT : W_AT + H]
-        b_all = small_all[:, B_AT : B_AT + H]
-        quantise_head(0)
-        bout_all = keep.tile([P, DOUT], F32)
-        nc.vector.tensor_copy(out=bout_all[:], in_=bout_ps[:])
-        shift = keep.tile([P, H], F32)
-        nc.vector.tensor_tensor(out=shift[:], in0=bprojT[:, 0:H], in1=w_all, op=ALU.mult)
-        nc.vector.tensor_tensor(out=coef[:, 0:H2], in0=coef[:, 0:H2], in1=w_all[:, 0:H2], op=ALU.mult)
-        nc.vector.tensor_tensor(out=shift[:], in0=shift[:], in1=b_all, op=ALU.add)
+        nc.gpsimd.dma_start(out=bproj[:, :, 0:PACK], in_=b_proj.rearrange("(g i) (q t) -> (i q) g t", g=PASSES, t=PACK))
+        ident = keep.tile([P, P], F32)
+        make_identity(nc, ident[:])
+        nc.gpsimd.dma_start(out=bout_all[:], in_=b_out.partition_broadcast(P))
+
+        V, S = nc.vector.tensor_copy, nc.scalar.copy
+        for h in range(3):
+            regroup_head(S, h, 0)
+            regroup_head(V, h, 1)
 
         x_words = x_sb[:].bitcast(F32).rearrange("r (c p u) -> r c u p", c=PASSES, p=P, u=2)
         for c in range(PASSES):
             for u in range(2):
-                nc.tensor.transpose(xT[:, c, u, :], x_words[:, c, u, :], ident_f32[:])
-        nc.scalar.copy(
+                nc.tensor.transpose(xT[:, c, u, :], x_words[:, c, u, :], ident[:])
+        for g in range(PASSES):
+            nc.tensor.matmul(
+                small_ps[:, g, 0:PER_HEAD],
+                lhsT=select[:, HEADS_PG * g : HEADS_PG * (g + 1), :].rearrange("h n q -> h (n q)"),
+                rhs=per_head[:, 0 : PER_HEAD * COLUMN_STEP : COLUMN_STEP],
+                start=True,
+                stop=True,
+            )
+        regroup_head(S, 3, 0)
+        regroup_head(V, 3, 1)
+        nc.vector.tensor_copy(
             out=x_grouped[:].bitcast(F32).rearrange("p (c r u) -> p c r u", c=PASSES, r=B, u=2),
             in_=xT[:].rearrange("p c u r -> p c r u"),
         )
-        for j in range(ROWS_PP):
-            nc.tensor.transpose(cachesT[:, j, :], caches_sb[:, j, :], ident_bf16[:])
-
-        regroup_head(2)
-        regroup_head(3)
-        quantise_head(1)
+        small = keep.tile([P, PASSES, PACK], F32)
+        nc.vector.tensor_copy(out=small[:, :, 0:PER_HEAD], in_=small_ps[:, :, 0:PER_HEAD])
+        clipped = keep.tile([P, PASSES], F32)
+        nc.gpsimd.tensor_scalar(
+            out=clipped[:], in0=small[:, :, DECAY_AT], scalar1=0.9, scalar2=1.0, op0=ALU.max, op1=ALU.min,
+        )
+        coef = keep.tile([P, PASSES], F32)
+        shift = keep.tile([P, PASSES, PACK], F32)
+        for g in range(PASSES):
+            nc.gpsimd.tensor_scalar(
+                out=shift[:, g, :], in0=bproj[:, g, 0:PACK],
+                scalar1=small[:, g, W_AT : W_AT + 1], scalar2=small[:, g, B_AT : B_AT + 1],
+                op0=ALU.mult, op1=ALU.add,
+            )
+        quantise_group(0, 0, 2)
+        regroup_head(S, 4, 0)
         nc.vector.quantize_mx(
             out=x_codes[:].rearrange("p c r -> p (c r)").bitcast(FP8X4),
             scales=x_scales[:].rearrange("p c r -> p (c r)"),
             in_=x_grouped[:],
         )
-        quantise_head(2)
-        for h in range(3):
-            project_head(h)
+        project(0, 0, 2)
+        quantise_group(0, 2, 4)
+        project(0, 2, 4)
+        regroup_head(S, 5, 0)
+        nc.scalar.activation(out=coef[:], in_=clipped[:], func=ACT.Sqrt)
+        nc.gpsimd.tensor_tensor(out=coef[:, 0:1], in0=coef[:, 0:1], in1=small[:, 0, W_AT : W_AT + 1], op=ALU.mult)
+        for h in (4, 5, 6):
+            regroup_head(V, h, 1)
+        regroup_head(S, 6, 0)
+        regroup_head(S, 7, 0)
+        regroup_head(S, 7, 1)
+        c_words = caches_sb[:].rearrange("r h k -> r (h k)").bitcast(F32).rearrange("r (g p u) -> r g u p", g=PASSES, p=P, u=2)
         for g in range(PASSES):
-            regroup_head(4 + 2 * g)
-            regroup_head(5 + 2 * g)
-            prepare_rest(g)
-            for h in (3 + 2 * g, 4 + 2 * g):
-                quantise_head(h)
-                project_head(h)
-
-        acc = [
-            psum.tile([P, HALF], F32, name="acc_left", tag="bank_left"),
-            psum.tile([P, HALF], F32, name="acc_right", tag="bank_right"),
-        ]
+            for u in range(2):
+                nc.tensor.transpose(cachesT[:, g, u, :], c_words[:, g, u, :], ident[:])
+        quantise_group(1, 0, 2)
+        project(1, 0, 2)
+        quantise_group(1, 2, 4)
+        project(1, 2, 4)
+        prepare_rest(0)
+        prepare_rest(1)
         mix(0)
-        regroup_w_out(0)
-        quantise_head(7)
-        project_head(7)
-        regroup(nc.vector.tensor_copy, hid_grouped[0][:], hid[0][:])
-        quantise_w_out(0, LEFT)
+        regroup_w_out(S, 0, 0, 320)
+        regroup_w_out(V, 0, 320, 512)
         quantise_hidden(0)
-        multiply(0, LEFT)
-        regroup_w_out(1)
+        regroup_w_out(S, 1, 0, 256)
+        regroup_w_out(V, 1, 384, 512)
         mix(1)
-        quantise_w_out(0, RIGHT)
+        quantise_w_out(0, 0, 512)
+        multiply(0, LEFT)
         multiply(0, RIGHT)
-        regroup(nc.vector.tensor_copy, hid_grouped[1][:], hid[1][:])
-        quantise_w_out(1, LEFT)
         quantise_hidden(1)
+        regroup_w_out(S, 1, 256, 384)
+        quantise_w_out(1, 0, 256)
         multiply(1, LEFT)
-        quantise_w_out(1, RIGHT)
+        quantise_w_out(1, 256, 512)
         multiply(1, RIGHT)
-
-        for half in (LEFT, RIGHT):
-            cols = slice(half * HALF, (half + 1) * HALF)
-            nc.vector.tensor_tensor(out=result[:, cols], in0=acc[half][:], in1=bout_all[:, cols], op=ALU.add)
-            nc.sync.dma_start(out=out[:, cols], in_=result[:, cols])
+        finish(LEFT)
+        finish(RIGHT)

@@ -38,6 +38,7 @@ def tile_mixedrepeatheads_s_kernel(
         psum = ctx.enter_context(tc.psum_pool(name="psum", bufs=1))
         ctx.enter_context(tc.manual_schedule())
 
+        bout_row = keep.tile([P, DOUT], BF16)
         bout_all = keep.tile([P, DOUT], BF16)
         per_head = keep.tile([P, PER_HEAD * COLUMN_STEP], BF16)
         bproj = keep.tile([P, PASSES, COLUMN_STEP], BF16)
@@ -67,6 +68,7 @@ def tile_mixedrepeatheads_s_kernel(
         xT = psum.tile([P, PASSES, 2, B], F32)
         cachesT = psum.tile([P, PASSES, 2, B], F32)
         small_ps = psum.tile([P, PASSES, PACK], F32)
+        bout_ps = psum.tile([P, DOUT], F32)
         projT = [psum.tile([P, PACK, B], F32, name="projT%d" % g) for g in range(PASSES)]
         acc = [psum.tile([P, HALF], F32, name="acc%d" % half) for half in (LEFT, RIGHT)]
 
@@ -182,6 +184,7 @@ def tile_mixedrepeatheads_s_kernel(
 
         warm = keep.tile([P, 1], F32)
         nc.vector.memset(warm[:], 1.0)
+        nc.vector.memset(bout_row[:], 0.0)
         nc.scalar.activation(out=warm[:], in_=warm[:], func=ACT.Sqrt)
         select = keep.tile([P, H, Q], BF16)
         nc.gpsimd.memset(select[:], 0.0)
@@ -192,7 +195,9 @@ def tile_mixedrepeatheads_s_kernel(
         nc.gpsimd.dma_start(out=bproj[:, :, 0:PACK], in_=b_proj.rearrange("(g i) (q t) -> (i q) g t", g=PASSES, t=PACK))
         ident = keep.tile([P, P], F32)
         make_identity(nc, ident[:])
-        nc.gpsimd.dma_start(out=bout_all[:], in_=b_out.partition_broadcast(P))
+        ones = keep.tile([P, P], BF16)
+        nc.gpsimd.memset(ones[:], 1.0)
+        nc.gpsimd.dma_start(out=bout_row[0:1, :], in_=b_out.rearrange("(o n) -> o n", o=1))
 
         V, S = nc.vector.tensor_copy, nc.scalar.copy
         for h in range(3):
@@ -249,6 +254,8 @@ def tile_mixedrepeatheads_s_kernel(
         regroup_head(S, 6, 0)
         regroup_head(S, 7, 0)
         regroup_head(S, 7, 1)
+        nc.tensor.matmul(bout_ps[:], lhsT=ones[:], rhs=bout_row[:], start=True, stop=True)
+        nc.scalar.copy(out=bout_all[:], in_=bout_ps[:])
         c_words = caches_sb[:].rearrange("r h k -> r (h k)").bitcast(F32).rearrange("r (g p u) -> r g u p", g=PASSES, p=P, u=2)
         for g in range(PASSES):
             for u in range(2):

@@ -38,10 +38,8 @@ def tile_mixedrepeatheads_s_kernel(
         psum = ctx.enter_context(tc.psum_pool(name="psum", bufs=1))
         ctx.enter_context(tc.manual_schedule())
 
-        bout_row = keep.tile([P, DOUT], BF16)
         bout_all = keep.tile([P, DOUT], BF16)
-        per_head = keep.tile([P, PER_HEAD * COLUMN_STEP], BF16)
-        bproj = keep.tile([P, PASSES, COLUMN_STEP], BF16)
+        vectors = keep.tile([P, DOUT + PER_HEAD * COLUMN_STEP], BF16)
         x_sb = keep.tile([P, DIM], BF16)
         wp_rows = [keep.tile([P, PASSES, PACK, HID], BF16, name="wp_rows%d" % h) for h in range(H)]
         caches_sb = keep.tile([P, H, HID], BF16)
@@ -67,7 +65,7 @@ def tile_mixedrepeatheads_s_kernel(
 
         xT = psum.tile([P, PASSES, 2, B], F32)
         cachesT = psum.tile([P, PASSES, 2, B], F32)
-        small_ps = psum.tile([P, PASSES, PACK], F32)
+        small_ps = psum.tile([P, PASSES * PER_HEAD + PACK * PASSES], F32)
         bout_ps = psum.tile([P, DOUT], F32)
         projT = [psum.tile([P, PACK, B], F32, name="projT%d" % g) for g in range(PASSES)]
         acc = [psum.tile([P, HALF], F32, name="acc%d" % half) for half in (LEFT, RIGHT)]
@@ -153,30 +151,30 @@ def tile_mixedrepeatheads_s_kernel(
             nc.vector.tensor_tensor(out=result[:, cols], in0=acc[half][:], in1=bout_all[:, cols], op=ALU.add)
             nc.sync.dma_start(out=out[:, cols], in_=result[:, cols])
 
-        nc.gpsimd.memset(per_head[:], 0.0)
+        nc.vector.memset(vectors[:].bitcast(F32), 0.0)
+        def load_head(h):
+            nc.sync.dma_start(
+                out=wp_rows[h][:].rearrange("p c j n -> p c (j n)"),
+                in_=W_proj[h].rearrange("(c p j) n -> p c (j n)", c=PASSES, p=P, j=PACK),
+            )
+
+        for h in range(3):
+            load_head(h)
+        nc.sync.dma_start(out=x_sb[:], in_=x)
+        load_head(3)
         per_head_sources = (
             w_mix[:, index : index + 1],
             b_mix[:, index : index + 1],
             decay_values.rearrange("(h o) -> h o", o=1),
         )
         for i in range(PER_HEAD):
-            nc.scalar.dma_start(
-                out=per_head[0:H, COLUMN_STEP * i : COLUMN_STEP * i + 1], in_=per_head_sources[i]
-            )
-
-        def load_head(h, c0=0, c1=PASSES):
             nc.sync.dma_start(
-                out=wp_rows[h][:, c0:c1].rearrange("p c j n -> p c (j n)"),
-                in_=W_proj[h].rearrange("(c p j) n -> p c (j n)", c=PASSES, p=P, j=PACK)[:, c0:c1, :],
+                out=vectors[0:H, DOUT + COLUMN_STEP * i : DOUT + COLUMN_STEP * i + 1], in_=per_head_sources[i]
             )
-
-        load_head(0, 0, 1)
-        load_head(0, 1, 2)
-        load_head(1)
-        load_head(2)
-        nc.sync.dma_start(out=x_sb[:], in_=x)
-        for h in range(3, H):
+        for h in range(4, H):
             load_head(h)
+        nc.sync.dma_start(out=vectors[HEADS_PG : HEADS_PG + PASSES, 0:DOUT], in_=b_proj.rearrange("(g i) k -> g (i k)", g=PASSES))
+        nc.sync.dma_start(out=vectors[0:HEADS_PG, 0:DOUT], in_=b_out.partition_broadcast(HEADS_PG))
         nc.sync.dma_start(out=caches_sb[:], in_=caches.rearrange("h r k -> r h k"))
         wo_view = W_out.rearrange("(g p j) n -> g p (j n)", g=PASSES, p=P, j=PACK)
         for g in range(PASSES):
@@ -184,7 +182,6 @@ def tile_mixedrepeatheads_s_kernel(
 
         warm = keep.tile([P, 1], F32)
         nc.vector.memset(warm[:], 1.0)
-        nc.vector.memset(bout_row[:], 0.0)
         nc.scalar.activation(out=warm[:], in_=warm[:], func=ACT.Sqrt)
         select = keep.tile([P, H, Q], BF16)
         nc.gpsimd.memset(select[:], 0.0)
@@ -192,12 +189,8 @@ def tile_mixedrepeatheads_s_kernel(
             out=select[:], in_=select[:], compare_op=ALU.not_equal, fill=1.0,
             base=0, pattern=[[-1, H], [0, Q]], channel_multiplier=1,
         )
-        nc.gpsimd.dma_start(out=bproj[:, :, 0:PACK], in_=b_proj.rearrange("(g i) (q t) -> (i q) g t", g=PASSES, t=PACK))
         ident = keep.tile([P, P], F32)
         make_identity(nc, ident[:])
-        ones = keep.tile([P, P], BF16)
-        nc.gpsimd.memset(ones[:], 1.0)
-        nc.gpsimd.dma_start(out=bout_row[0:1, :], in_=b_out.rearrange("(o n) -> o n", o=1))
 
         V, S = nc.vector.tensor_copy, nc.scalar.copy
         for h in range(3):
@@ -210,9 +203,9 @@ def tile_mixedrepeatheads_s_kernel(
                 nc.tensor.transpose(xT[:, c, u, :], x_words[:, c, u, :], ident[:])
         for g in range(PASSES):
             nc.tensor.matmul(
-                small_ps[:, g, 0:PER_HEAD],
+                small_ps[:, PER_HEAD * g : PER_HEAD * (g + 1)],
                 lhsT=select[:, HEADS_PG * g : HEADS_PG * (g + 1), :].rearrange("h n q -> h (n q)"),
-                rhs=per_head[:, 0 : PER_HEAD * COLUMN_STEP : COLUMN_STEP],
+                rhs=vectors[:, DOUT : DOUT + PER_HEAD * COLUMN_STEP : COLUMN_STEP],
                 start=True,
                 stop=True,
             )
@@ -222,26 +215,33 @@ def tile_mixedrepeatheads_s_kernel(
             out=x_grouped[:].bitcast(F32).rearrange("p (c r u) -> p c r u", c=PASSES, r=B, u=2),
             in_=xT[:].rearrange("p c u r -> p c r u"),
         )
-        small = keep.tile([P, PASSES, PACK], F32)
-        nc.vector.tensor_copy(out=small[:, :, 0:PER_HEAD], in_=small_ps[:, :, 0:PER_HEAD])
+        small = keep.tile([P, PASSES, PER_HEAD], F32)
+        nc.vector.tensor_copy(out=small[:].rearrange("p g i -> p (g i)"), in_=small_ps[:, 0 : PASSES * PER_HEAD])
         clipped = keep.tile([P, PASSES], F32)
         nc.gpsimd.tensor_scalar(
             out=clipped[:], in0=small[:, :, DECAY_AT], scalar1=0.9, scalar2=1.0, op0=ALU.max, op1=ALU.min,
         )
         coef = keep.tile([P, PASSES], F32)
         shift = keep.tile([P, PASSES, PACK], F32)
-        for g in range(PASSES):
-            nc.gpsimd.tensor_scalar(
-                out=shift[:, g, :], in0=bproj[:, g, 0:PACK],
-                scalar1=small[:, g, W_AT : W_AT + 1], scalar2=small[:, g, B_AT : B_AT + 1],
-                op0=ALU.mult, op1=ALU.add,
-            )
         quantise_group(0, 0, 2)
         regroup_head(S, 4, 0)
         nc.vector.quantize_mx(
             out=x_codes[:].rearrange("p c r -> p (c r)").bitcast(FP8X4),
             scales=x_scales[:].rearrange("p c r -> p (c r)"),
             in_=x_grouped[:],
+        )
+        for t in range(PACK):
+            at = PASSES * PER_HEAD + PASSES * t
+            nc.tensor.matmul(
+                small_ps[:, at : at + PASSES],
+                lhsT=vectors[:, t:DOUT:PACK],
+                rhs=select[:, HEADS_PG : HEADS_PG + PASSES, 0],
+                start=True,
+                stop=True,
+            )
+        nc.tensor.matmul(
+            bout_ps[:], lhsT=select[:, 0:HEADS_PG, :].rearrange("h n q -> h (n q)"), rhs=vectors[:, 0:DOUT],
+            start=True, stop=True,
         )
         project(0, 0, 2)
         quantise_group(0, 2, 4)
@@ -251,10 +251,17 @@ def tile_mixedrepeatheads_s_kernel(
         nc.gpsimd.tensor_tensor(out=coef[:, 0:1], in0=coef[:, 0:1], in1=small[:, 0, W_AT : W_AT + 1], op=ALU.mult)
         for h in (4, 5, 6):
             regroup_head(V, h, 1)
+        bproj = keep.tile([P, PACK, PASSES], F32)
+        nc.vector.tensor_copy(out=bproj[:].rearrange("p t g -> p (t g)"), in_=small_ps[:, PASSES * PER_HEAD :])
+        for g in range(PASSES):
+            nc.gpsimd.tensor_scalar(
+                out=shift[:, g, :], in0=bproj[:, :, g],
+                scalar1=small[:, g, W_AT : W_AT + 1], scalar2=small[:, g, B_AT : B_AT + 1],
+                op0=ALU.mult, op1=ALU.add,
+            )
         regroup_head(S, 6, 0)
         regroup_head(S, 7, 0)
         regroup_head(S, 7, 1)
-        nc.tensor.matmul(bout_ps[:], lhsT=ones[:], rhs=bout_row[:], start=True, stop=True)
         nc.scalar.copy(out=bout_all[:], in_=bout_ps[:])
         c_words = caches_sb[:].rearrange("r h k -> r (h k)").bitcast(F32).rearrange("r (g p u) -> r g u p", g=PASSES, p=P, u=2)
         for g in range(PASSES):

@@ -158,10 +158,8 @@ def tile_mixedrepeatheads_s_kernel(
                 in_=W_proj[h].rearrange("(c p j) n -> p c (j n)", c=PASSES, p=P, j=PACK),
             )
 
-        for h in range(3):
+        for h in range(4):
             load_head(h)
-        nc.sync.dma_start(out=x_sb[:], in_=x)
-        load_head(3)
         per_head_sources = (
             w_mix[:, index : index + 1],
             b_mix[:, index : index + 1],
@@ -171,14 +169,17 @@ def tile_mixedrepeatheads_s_kernel(
             nc.sync.dma_start(
                 out=vectors[0:H, DOUT + COLUMN_STEP * i : DOUT + COLUMN_STEP * i + 1], in_=per_head_sources[i]
             )
-        for h in range(4, H):
-            load_head(h)
+        load_head(4)
+        nc.sync.dma_start(out=x_sb[:], in_=x)
+        load_head(5)
         nc.sync.dma_start(out=vectors[HEADS_PG : HEADS_PG + PASSES, 0:DOUT], in_=b_proj.rearrange("(g i) k -> g (i k)", g=PASSES))
         nc.sync.dma_start(out=vectors[0:HEADS_PG, 0:DOUT], in_=b_out.partition_broadcast(HEADS_PG))
-        nc.sync.dma_start(out=caches_sb[:], in_=caches.rearrange("h r k -> r h k"))
+        load_head(6)
+        load_head(7)
         wo_view = W_out.rearrange("(g p j) n -> g p (j n)", g=PASSES, p=P, j=PACK)
-        for g in range(PASSES):
-            nc.sync.dma_start(out=wo_rows[g][:].rearrange("p j n -> p (j n)"), in_=wo_view[g])
+        nc.sync.dma_start(out=wo_rows[0][:].rearrange("p j n -> p (j n)"), in_=wo_view[0])
+        nc.sync.dma_start(out=caches_sb[:], in_=caches.rearrange("h r k -> r h k"))
+        nc.sync.dma_start(out=wo_rows[1][:].rearrange("p j n -> p (j n)"), in_=wo_view[1])
 
         warm = keep.tile([P, 1], F32)
         nc.vector.memset(warm[:], 1.0)
@@ -193,14 +194,9 @@ def tile_mixedrepeatheads_s_kernel(
         make_identity(nc, ident[:])
 
         V, S = nc.vector.tensor_copy, nc.scalar.copy
-        for h in range(3):
+        for h in range(4):
             regroup_head(S, h, 0)
             regroup_head(V, h, 1)
-
-        x_words = x_sb[:].bitcast(F32).rearrange("r (c p u) -> r c u p", c=PASSES, p=P, u=2)
-        for c in range(PASSES):
-            for u in range(2):
-                nc.tensor.transpose(xT[:, c, u, :], x_words[:, c, u, :], ident[:])
         for g in range(PASSES):
             nc.tensor.matmul(
                 small_ps[:, PER_HEAD * g : PER_HEAD * (g + 1)],
@@ -209,12 +205,6 @@ def tile_mixedrepeatheads_s_kernel(
                 start=True,
                 stop=True,
             )
-        regroup_head(S, 3, 0)
-        regroup_head(V, 3, 1)
-        nc.vector.tensor_copy(
-            out=x_grouped[:].bitcast(F32).rearrange("p (c r u) -> p c r u", c=PASSES, r=B, u=2),
-            in_=xT[:].rearrange("p c u r -> p c r u"),
-        )
         small = keep.tile([P, PASSES, PER_HEAD], F32)
         nc.vector.tensor_copy(out=small[:].rearrange("p g i -> p (g i)"), in_=small_ps[:, 0 : PASSES * PER_HEAD])
         clipped = keep.tile([P, PASSES], F32)
@@ -223,13 +213,29 @@ def tile_mixedrepeatheads_s_kernel(
         )
         coef = keep.tile([P, PASSES], F32)
         shift = keep.tile([P, PASSES, PACK], F32)
-        quantise_group(0, 0, 2)
         regroup_head(S, 4, 0)
+        quantise_group(0, 0, 2)
+        regroup_head(V, 4, 1)
+        quantise_group(0, 2, 4)
+        regroup_head(S, 5, 0)
+        nc.scalar.activation(out=coef[:], in_=clipped[:], func=ACT.Sqrt)
+        nc.gpsimd.tensor_tensor(out=coef[:, 0:1], in0=coef[:, 0:1], in1=small[:, 0, W_AT : W_AT + 1], op=ALU.mult)
+
+        x_words = x_sb[:].bitcast(F32).rearrange("r (c p u) -> r c u p", c=PASSES, p=P, u=2)
+        for c in range(PASSES):
+            for u in range(2):
+                nc.tensor.transpose(xT[:, c, u, :], x_words[:, c, u, :], ident[:])
+        nc.vector.tensor_copy(
+            out=x_grouped[:].bitcast(F32).rearrange("p (c r u) -> p c r u", c=PASSES, r=B, u=2),
+            in_=xT[:].rearrange("p c u r -> p c r u"),
+        )
+        regroup_head(V, 5, 1)
         nc.vector.quantize_mx(
             out=x_codes[:].rearrange("p c r -> p (c r)").bitcast(FP8X4),
             scales=x_scales[:].rearrange("p c r -> p (c r)"),
             in_=x_grouped[:],
         )
+        regroup_head(S, 6, 0)
         for t in range(PACK):
             at = PASSES * PER_HEAD + PASSES * t
             nc.tensor.matmul(
@@ -244,13 +250,8 @@ def tile_mixedrepeatheads_s_kernel(
             start=True, stop=True,
         )
         project(0, 0, 2)
-        quantise_group(0, 2, 4)
         project(0, 2, 4)
-        regroup_head(S, 5, 0)
-        nc.scalar.activation(out=coef[:], in_=clipped[:], func=ACT.Sqrt)
-        nc.gpsimd.tensor_tensor(out=coef[:, 0:1], in0=coef[:, 0:1], in1=small[:, 0, W_AT : W_AT + 1], op=ALU.mult)
-        for h in (4, 5, 6):
-            regroup_head(V, h, 1)
+        regroup_head(V, 6, 1)
         bproj = keep.tile([P, PACK, PASSES], F32)
         nc.vector.tensor_copy(out=bproj[:].rearrange("p t g -> p (t g)"), in_=small_ps[:, PASSES * PER_HEAD :])
         for g in range(PASSES):
@@ -259,35 +260,32 @@ def tile_mixedrepeatheads_s_kernel(
                 scalar1=small[:, g, W_AT : W_AT + 1], scalar2=small[:, g, B_AT : B_AT + 1],
                 op0=ALU.mult, op1=ALU.add,
             )
-        regroup_head(S, 6, 0)
         regroup_head(S, 7, 0)
-        regroup_head(S, 7, 1)
+        regroup_head(V, 7, 1)
         nc.scalar.copy(out=bout_all[:], in_=bout_ps[:])
+        quantise_group(1, 0, 2)
+        quantise_group(1, 2, 4)
+        regroup_w_out(S, 0, 0, 384)
         c_words = caches_sb[:].rearrange("r h k -> r (h k)").bitcast(F32).rearrange("r (g p u) -> r g u p", g=PASSES, p=P, u=2)
         for g in range(PASSES):
             for u in range(2):
                 nc.tensor.transpose(cachesT[:, g, u, :], c_words[:, g, u, :], ident[:])
-        quantise_group(1, 0, 2)
-        project(1, 0, 2)
-        quantise_group(1, 2, 4)
-        project(1, 2, 4)
+        project(1, 0, 4)
         prepare_rest(0)
+        regroup_w_out(V, 0, 384, 512)
+        regroup_w_out(V, 1, 256, 512)
         prepare_rest(1)
-        mix(0)
-        regroup_w_out(S, 0, 0, 320)
-        regroup_w_out(V, 0, 320, 512)
-        quantise_hidden(0)
-        regroup_w_out(S, 1, 0, 256)
-        regroup_w_out(V, 1, 384, 512)
-        mix(1)
         quantise_w_out(0, 0, 512)
+        mix(0)
+        quantise_w_out(1, 256, 512)
+        quantise_hidden(0)
         multiply(0, LEFT)
         multiply(0, RIGHT)
-        quantise_hidden(1)
-        regroup_w_out(S, 1, 256, 384)
+        regroup_w_out(S, 1, 0, 256)
+        mix(1)
         quantise_w_out(1, 0, 256)
-        multiply(1, LEFT)
-        quantise_w_out(1, 256, 512)
+        quantise_hidden(1)
         multiply(1, RIGHT)
-        finish(LEFT)
+        multiply(1, LEFT)
         finish(RIGHT)
+        finish(LEFT)

@@ -63,10 +63,9 @@ def tile_mixedrepeatheads_s_kernel(
         wo_scales = [keep.tile([P, DOUT], U8, name="wo_scales%d" % g, align_bytes=64) for g in range(PASSES)]
         result = keep.tile([P, DOUT], F32)
 
-        xT = psum.tile([P, PASSES, 2, B], F32)
-        cachesT = psum.tile([P, PASSES, 2, B], F32)
+        xT = psum.tile([P, PASSES, 2, B], F32, tag="bank_x")
         small_ps = psum.tile([P, PASSES * PER_HEAD + PACK * PASSES], F32)
-        bout_ps = psum.tile([P, DOUT], F32)
+        bout_ps = psum.tile([P, DOUT], BF16)
         projT = [psum.tile([P, PACK, B], F32, name="projT%d" % g) for g in range(PASSES)]
         acc = [psum.tile([P, HALF], F32, name="acc%d" % half) for half in (LEFT, RIGHT)]
 
@@ -99,7 +98,7 @@ def tile_mixedrepeatheads_s_kernel(
 
         def prepare_rest(g):
             for u in range(2):
-                pair = cachesT[:, g, u, :].bitcast(BF16).rearrange("p (r e) -> p e r", e=2)
+                pair = cachesT[g][:, u, :].bitcast(BF16).rearrange("p (r e) -> p e r", e=2)
                 for e in range(2):
                     t = 2 * u + e
                     nc.scalar.activation(
@@ -261,31 +260,36 @@ def tile_mixedrepeatheads_s_kernel(
                 op0=ALU.mult, op1=ALU.add,
             )
         regroup_head(S, 7, 0)
-        regroup_head(V, 7, 1)
+        regroup_head(S, 7, 1)
         nc.scalar.copy(out=bout_all[:], in_=bout_ps[:])
         quantise_group(1, 0, 2)
         quantise_group(1, 2, 4)
-        regroup_w_out(S, 0, 0, 384)
+        regroup_w_out(S, 0, 0, 320)
+        regroup_w_out(V, 0, 320, 512)
         c_words = caches_sb[:].rearrange("r h k -> r (h k)").bitcast(F32).rearrange("r (g p u) -> r g u p", g=PASSES, p=P, u=2)
+        cachesT = [
+            psum.tile([P, 2, B], F32, name="cachesT0", tag="bank_caches"),
+            psum.tile([P, 2, B], F32, name="cachesT1", tag="bank_x"),
+        ]
         for g in range(PASSES):
             for u in range(2):
-                nc.tensor.transpose(cachesT[:, g, u, :], c_words[:, g, u, :], ident[:])
+                nc.tensor.transpose(cachesT[g][:, u, :], c_words[:, g, u, :], ident[:])
         project(1, 0, 4)
         prepare_rest(0)
-        regroup_w_out(V, 0, 384, 512)
-        regroup_w_out(V, 1, 256, 512)
         prepare_rest(1)
         quantise_w_out(0, 0, 512)
         mix(0)
-        quantise_w_out(1, 256, 512)
+        regroup_w_out(S, 1, 0, 256)
+        regroup_w_out(V, 1, 320, 512)
         quantise_hidden(0)
         multiply(0, LEFT)
         multiply(0, RIGHT)
-        regroup_w_out(S, 1, 0, 256)
         mix(1)
+        regroup_w_out(S, 1, 256, 320)
         quantise_w_out(1, 0, 256)
         quantise_hidden(1)
-        multiply(1, RIGHT)
         multiply(1, LEFT)
-        finish(RIGHT)
+        quantise_w_out(1, 256, 512)
+        multiply(1, RIGHT)
         finish(LEFT)
+        finish(RIGHT)

@@ -41,7 +41,8 @@ def tile_mixedrepeatheads_s_kernel(
         bout_all = keep.tile([P, DOUT], BF16)
         vectors = keep.tile([P, DOUT + PER_HEAD * COLUMN_STEP], BF16)
         x_sb = keep.tile([P, DIM], BF16)
-        wp_rows = [keep.tile([P, PASSES, PACK, HID], BF16, name="wp_rows%d" % h) for h in range(H)]
+        pieces = [(g, c, pair) for g in range(PASSES) for c in range(PASSES) for pair in range(HEADS_PG // 2)]
+        wp_rows = {piece: keep.tile([P, 2, PACK, HID], BF16, name="wp_rows%d%d%d" % piece) for piece in pieces}
         caches_sb = keep.tile([P, H, HID], BF16)
         wo_rows = [keep.tile([P, PACK, DOUT], BF16, name="wo_rows%d" % g) for g in range(PASSES)]
 
@@ -49,11 +50,11 @@ def tile_mixedrepeatheads_s_kernel(
         x_codes = keep.tile([P, PASSES, B], U32, align_bytes=64)
         x_scales = keep.tile([P, PASSES, B], U8, align_bytes=64)
         wp_grouped = [
-            keep.tile([P, PACK, PASSES, HEADS_PG, Q, PACK], BF16, name="wp_grouped%d" % g, align_bytes=64)
+            keep.tile([P, PASSES, PACK, HEADS_PG, Q, PACK], BF16, name="wp_grouped%d" % g, align_bytes=64)
             for g in range(PASSES)
         ]
-        wp_codes = [keep.tile([P, PACK, PASSES, P], U32, name="wp_codes%d" % g, align_bytes=64) for g in range(PASSES)]
-        wp_scales = [keep.tile([P, PACK, PASSES, P], U8, name="wp_scales%d" % g, align_bytes=64) for g in range(PASSES)]
+        wp_codes = [keep.tile([P, PASSES, PACK, P], U32, name="wp_codes%d" % g, align_bytes=64) for g in range(PASSES)]
+        wp_scales = [keep.tile([P, PASSES, PACK, P], U8, name="wp_scales%d" % g, align_bytes=64) for g in range(PASSES)]
         rest = [keep.tile([P, PACK, B], F32, name="rest%d" % g) for g in range(PASSES)]
         hid_grouped = [keep.tile([P, B, PACK], BF16, name="hid_grouped%d" % g, align_bytes=64) for g in range(PASSES)]
         hid_codes = [keep.tile([P, B], U32, name="hid_codes%d" % g, align_bytes=64) for g in range(PASSES)]
@@ -69,27 +70,27 @@ def tile_mixedrepeatheads_s_kernel(
         projT = [psum.tile([P, PACK, B], F32, name="projT%d" % g) for g in range(PASSES)]
         acc = [psum.tile([P, HALF], F32, name="acc%d" % half) for half in (LEFT, RIGHT)]
 
-        def regroup_head(copy, h, c):
-            g, i = divmod(h, HEADS_PG)
+        def regroup_head(copy, piece, head):
+            g, c, pair = pieces[piece]
             copy(
-                out=wp_grouped[g][:, :, c, i, :, :].rearrange("p t q j -> p q j t"),
-                in_=wp_rows[h][:, c, :, :].rearrange("p j (q t) -> p q j t", t=PACK),
+                out=wp_grouped[g][:, c, :, 2 * pair + head, :, :].rearrange("p t q j -> p q j t"),
+                in_=wp_rows[pieces[piece]][:, head, :, :].rearrange("p j (q t) -> p q j t", t=PACK),
             )
 
-        def quantise_group(g, t0, t1):
+        def quantise_group(g, c):
             nc.vector.quantize_mx(
-                out=wp_codes[g][:, t0:t1].rearrange("p t c m -> p (t c m)").bitcast(FP8X4),
-                scales=wp_scales[g][:, t0:t1].rearrange("p t c m -> p (t c m)"),
-                in_=wp_grouped[g][:, t0:t1].rearrange("p t c i q j -> p (t c i q j)"),
+                out=wp_codes[g][:, c].rearrange("p t m -> p (t m)").bitcast(FP8X4),
+                scales=wp_scales[g][:, c].rearrange("p t m -> p (t m)"),
+                in_=wp_grouped[g][:, c].rearrange("p t i q j -> p (t i q j)"),
             )
 
-        def project(g, t0, t1):
-            for t in range(t0, t1):
+        def project(g):
+            for t in range(PACK):
                 for c in range(PASSES):
                     nc.tensor.matmul_mx(
                         out=projT[g][:, t, :],
-                        lhsT=wp_codes[g][:, t, c, :].bitcast(FP8X4),
-                        lhsT_scale=wp_scales[g][:, t, c, :],
+                        lhsT=wp_codes[g][:, c, t, :].bitcast(FP8X4),
+                        lhsT_scale=wp_scales[g][:, c, t, :],
                         rhs=x_codes[:, c, :].bitcast(FP8X4),
                         rhs_scale=x_scales[:, c, :],
                         start=(c == 0),
@@ -151,14 +152,16 @@ def tile_mixedrepeatheads_s_kernel(
             nc.sync.dma_start(out=out[:, cols], in_=result[:, cols])
 
         nc.vector.memset(vectors[:].bitcast(F32), 0.0)
-        def load_head(h):
+        def load_piece(piece):
+            g, c, pair = pieces[piece]
+            h = HEADS_PG * g + 2 * pair
             nc.sync.dma_start(
-                out=wp_rows[h][:].rearrange("p c j n -> p c (j n)"),
-                in_=W_proj[h].rearrange("(c p j) n -> p c (j n)", c=PASSES, p=P, j=PACK),
+                out=wp_rows[pieces[piece]][:].rearrange("p i j n -> p i (j n)"),
+                in_=W_proj[h : h + 2, K_PASS * c : K_PASS * (c + 1), :].rearrange("i (p j) n -> p i (j n)", j=PACK),
             )
 
         for h in range(4):
-            load_head(h)
+            load_piece(h)
         per_head_sources = (
             w_mix[:, index : index + 1],
             b_mix[:, index : index + 1],
@@ -168,13 +171,13 @@ def tile_mixedrepeatheads_s_kernel(
             nc.sync.dma_start(
                 out=vectors[0:H, DOUT + COLUMN_STEP * i : DOUT + COLUMN_STEP * i + 1], in_=per_head_sources[i]
             )
-        load_head(4)
+        load_piece(4)
         nc.sync.dma_start(out=x_sb[:], in_=x)
-        load_head(5)
+        load_piece(5)
         nc.sync.dma_start(out=vectors[HEADS_PG : HEADS_PG + PASSES, 0:DOUT], in_=b_proj.rearrange("(g i) k -> g (i k)", g=PASSES))
         nc.sync.dma_start(out=vectors[0:HEADS_PG, 0:DOUT], in_=b_out.partition_broadcast(HEADS_PG))
-        load_head(6)
-        load_head(7)
+        load_piece(6)
+        load_piece(7)
         wo_view = W_out.rearrange("(g p j) n -> g p (j n)", g=PASSES, p=P, j=PACK)
         nc.sync.dma_start(out=wo_rows[0][:].rearrange("p j n -> p (j n)"), in_=wo_view[0])
         nc.sync.dma_start(out=caches_sb[:], in_=caches.rearrange("h r k -> r h k"))
@@ -193,9 +196,12 @@ def tile_mixedrepeatheads_s_kernel(
         make_identity(nc, ident[:])
 
         V, S = nc.vector.tensor_copy, nc.scalar.copy
-        for h in range(4):
-            regroup_head(S, h, 0)
-            regroup_head(V, h, 1)
+        for n in range(3):
+            regroup_head(S, n, 0)
+            regroup_head(V, n, 1)
+        quantise_group(0, 0)
+        regroup_head(S, 3, 0)
+        regroup_head(V, 3, 1)
         for g in range(PASSES):
             nc.tensor.matmul(
                 small_ps[:, PER_HEAD * g : PER_HEAD * (g + 1)],
@@ -213,10 +219,10 @@ def tile_mixedrepeatheads_s_kernel(
         coef = keep.tile([P, PASSES], F32)
         shift = keep.tile([P, PASSES, PACK], F32)
         regroup_head(S, 4, 0)
-        quantise_group(0, 0, 2)
         regroup_head(V, 4, 1)
-        quantise_group(0, 2, 4)
+        quantise_group(0, 1)
         regroup_head(S, 5, 0)
+        regroup_head(V, 5, 1)
         nc.scalar.activation(out=coef[:], in_=clipped[:], func=ACT.Sqrt)
         nc.gpsimd.tensor_tensor(out=coef[:, 0:1], in0=coef[:, 0:1], in1=small[:, 0, W_AT : W_AT + 1], op=ALU.mult)
 
@@ -228,7 +234,7 @@ def tile_mixedrepeatheads_s_kernel(
             out=x_grouped[:].bitcast(F32).rearrange("p (c r u) -> p c r u", c=PASSES, r=B, u=2),
             in_=xT[:].rearrange("p c u r -> p c r u"),
         )
-        regroup_head(V, 5, 1)
+        regroup_head(V, 6, 1)
         nc.vector.quantize_mx(
             out=x_codes[:].rearrange("p c r -> p (c r)").bitcast(FP8X4),
             scales=x_scales[:].rearrange("p c r -> p (c r)"),
@@ -248,9 +254,8 @@ def tile_mixedrepeatheads_s_kernel(
             bout_ps[:], lhsT=select[:, 0:HEADS_PG, :].rearrange("h n q -> h (n q)"), rhs=vectors[:, 0:DOUT],
             start=True, stop=True,
         )
-        project(0, 0, 2)
-        project(0, 2, 4)
-        regroup_head(V, 6, 1)
+        project(0)
+        quantise_group(1, 0)
         bproj = keep.tile([P, PACK, PASSES], F32)
         nc.vector.tensor_copy(out=bproj[:].rearrange("p t g -> p (t g)"), in_=small_ps[:, PASSES * PER_HEAD :])
         for g in range(PASSES):
@@ -262,8 +267,7 @@ def tile_mixedrepeatheads_s_kernel(
         regroup_head(S, 7, 0)
         regroup_head(S, 7, 1)
         nc.scalar.copy(out=bout_all[:], in_=bout_ps[:])
-        quantise_group(1, 0, 2)
-        quantise_group(1, 2, 4)
+        quantise_group(1, 1)
         regroup_w_out(S, 0, 0, 320)
         regroup_w_out(V, 0, 320, 512)
         c_words = caches_sb[:].rearrange("r h k -> r (h k)").bitcast(F32).rearrange("r (g p u) -> r g u p", g=PASSES, p=P, u=2)
@@ -274,7 +278,7 @@ def tile_mixedrepeatheads_s_kernel(
         for g in range(PASSES):
             for u in range(2):
                 nc.tensor.transpose(cachesT[g][:, u, :], c_words[:, g, u, :], ident[:])
-        project(1, 0, 4)
+        project(1)
         prepare_rest(0)
         prepare_rest(1)
         quantise_w_out(0, 0, 512)

@@ -213,7 +213,7 @@ def tile_mixedrepeatheads_s_kernel(
         small = keep.tile([P, PASSES, PER_HEAD], F32)
         nc.vector.tensor_copy(out=small[:].rearrange("p g i -> p (g i)"), in_=small_ps[:, 0 : PASSES * PER_HEAD])
         clipped = keep.tile([P, PASSES], F32)
-        nc.gpsimd.tensor_scalar(
+        nc.vector.tensor_scalar(
             out=clipped[:], in0=small[:, :, DECAY_AT], scalar1=0.9, scalar2=1.0, op0=ALU.max, op1=ALU.min,
         )
         coef = keep.tile([P, PASSES], F32)
@@ -221,10 +221,10 @@ def tile_mixedrepeatheads_s_kernel(
         regroup_head(S, 4, 0)
         regroup_head(V, 4, 1)
         quantise_group(0, 1)
+        nc.scalar.activation(out=coef[:], in_=clipped[:], func=ACT.Sqrt)
         regroup_head(S, 5, 0)
         regroup_head(V, 5, 1)
-        nc.scalar.activation(out=coef[:], in_=clipped[:], func=ACT.Sqrt)
-        nc.gpsimd.tensor_tensor(out=coef[:, 0:1], in0=coef[:, 0:1], in1=small[:, 0, W_AT : W_AT + 1], op=ALU.mult)
+        nc.vector.tensor_tensor(out=coef[:, 0:1], in0=coef[:, 0:1], in1=small[:, 0, W_AT : W_AT + 1], op=ALU.mult)
 
         x_words = x_sb[:].bitcast(F32).rearrange("r (c p u) -> r c u p", c=PASSES, p=P, u=2)
         for c in range(PASSES):
@@ -256,11 +256,10 @@ def tile_mixedrepeatheads_s_kernel(
         )
         project(0)
         quantise_group(1, 0)
-        bproj = keep.tile([P, PACK, PASSES], F32)
-        nc.vector.tensor_copy(out=bproj[:].rearrange("p t g -> p (t g)"), in_=small_ps[:, PASSES * PER_HEAD :])
+        bproj = small_ps[:, PASSES * PER_HEAD :].rearrange("p (t g) -> p g t", g=PASSES)
         for g in range(PASSES):
-            nc.gpsimd.tensor_scalar(
-                out=shift[:, g, :], in0=bproj[:, :, g],
+            nc.vector.tensor_scalar(
+                out=shift[:, g, :], in0=bproj[:, g, :],
                 scalar1=small[:, g, W_AT : W_AT + 1], scalar2=small[:, g, B_AT : B_AT + 1],
                 op0=ALU.mult, op1=ALU.add,
             )

@@ -250,10 +250,11 @@ def tile_mixedrepeatheads_s_kernel(
                 start=True,
                 stop=True,
             )
-        nc.tensor.matmul(
-            bout_ps[:], lhsT=select[:, 0:HEADS_PG, :].rearrange("h n q -> h (n q)"), rhs=vectors[:, 0:DOUT],
-            start=True, stop=True,
-        )
+        for repeat in range(2):
+            nc.tensor.matmul(
+                bout_ps[:], lhsT=select[:, 0:HEADS_PG, :].rearrange("h n q -> h (n q)"), rhs=vectors[:, 0:DOUT],
+                start=True, stop=True,
+            )
         project(0)
         quantise_group(1, 0)
         bproj = small_ps[:, PASSES * PER_HEAD :].rearrange("p (t g) -> p g t", g=PASSES)
@@ -267,8 +268,8 @@ def tile_mixedrepeatheads_s_kernel(
         regroup_head(S, 7, 1)
         nc.scalar.copy(out=bout_all[:], in_=bout_ps[:])
         quantise_group(1, 1)
-        regroup_w_out(S, 0, 0, 320)
-        regroup_w_out(V, 0, 320, 512)
+        regroup_w_out(S, 0, 0, 256)
+        regroup_w_out(V, 0, 256, 512)
         c_words = caches_sb[:].rearrange("r h k -> r (h k)").bitcast(F32).rearrange("r (g p u) -> r g u p", g=PASSES, p=P, u=2)
         cachesT = [
             psum.tile([P, 2, B], F32, name="cachesT0", tag="bank_caches"),
@@ -280,7 +281,8 @@ def tile_mixedrepeatheads_s_kernel(
         project(1)
         prepare_rest(0)
         prepare_rest(1)
-        quantise_w_out(0, 0, 512)
+        quantise_w_out(0, 0, 256)
+        quantise_w_out(0, 256, 512)
         mix(0)
         regroup_w_out(S, 1, 0, 256)
         regroup_w_out(V, 1, 320, 512)

@@ -43,7 +43,7 @@ def tile_mixedrepeatheads_s_kernel(
         x_sb = keep.tile([P, DIM], BF16)
         pieces = [(g, c, pair) for g in range(PASSES) for c in range(PASSES) for pair in range(HEADS_PG // 2)]
         wp_rows = {piece: keep.tile([P, 2, PACK, HID], BF16, name="wp_rows%d%d%d" % piece) for piece in pieces}
-        caches_sb = keep.tile([P, H, HID], BF16)
+        caches_sb = [keep.tile([P, HEADS_PG, HID], BF16, name="caches_sb%d" % g) for g in range(PASSES)]
         wo_rows = [keep.tile([P, PACK, DOUT], BF16, name="wo_rows%d" % g) for g in range(PASSES)]
 
         x_grouped = keep.tile([P, PASSES * B * PACK], BF16, align_bytes=64)
@@ -180,7 +180,10 @@ def tile_mixedrepeatheads_s_kernel(
         load_piece(7)
         wo_view = W_out.rearrange("(g p j) n -> g p (j n)", g=PASSES, p=P, j=PACK)
         nc.sync.dma_start(out=wo_rows[0][:].rearrange("p j n -> p (j n)"), in_=wo_view[0])
-        nc.sync.dma_start(out=caches_sb[:], in_=caches.rearrange("h r k -> r h k"))
+        for g in range(PASSES):
+            nc.sync.dma_start(
+                out=caches_sb[g][:], in_=caches[HEADS_PG * g : HEADS_PG * (g + 1)].rearrange("h r k -> r h k")
+            )
         nc.sync.dma_start(out=wo_rows[1][:].rearrange("p j n -> p (j n)"), in_=wo_view[1])
 
         warm = keep.tile([P, 1], F32)
@@ -266,31 +269,34 @@ def tile_mixedrepeatheads_s_kernel(
             )
         regroup_head(S, 7, 0)
         regroup_head(S, 7, 1)
-        nc.scalar.copy(out=bout_all[:], in_=bout_ps[:])
         quantise_group(1, 1)
         regroup_w_out(S, 0, 0, 256)
         regroup_w_out(V, 0, 256, 512)
-        c_words = caches_sb[:].rearrange("r h k -> r (h k)").bitcast(F32).rearrange("r (g p u) -> r g u p", g=PASSES, p=P, u=2)
+        c_words = [
+            caches_sb[g][:].rearrange("r h k -> r (h k)").bitcast(F32).rearrange("r (p u) -> r u p", u=2)
+            for g in range(PASSES)
+        ]
         cachesT = [
             psum.tile([P, 2, B], F32, name="cachesT0", tag="bank_caches"),
             psum.tile([P, 2, B], F32, name="cachesT1", tag="bank_x"),
         ]
         for g in range(PASSES):
             for u in range(2):
-                nc.tensor.transpose(cachesT[g][:, u, :], c_words[:, g, u, :], ident[:])
+                nc.tensor.transpose(cachesT[g][:, u, :], c_words[g][:, u, :], ident[:])
         project(1)
+        nc.scalar.copy(out=bout_all[:], in_=bout_ps[:])
         prepare_rest(0)
         prepare_rest(1)
         quantise_w_out(0, 0, 256)
         quantise_w_out(0, 256, 512)
         mix(0)
         regroup_w_out(S, 1, 0, 256)
-        regroup_w_out(V, 1, 320, 512)
+        regroup_w_out(V, 1, 384, 512)
         quantise_hidden(0)
         multiply(0, LEFT)
         multiply(0, RIGHT)
         mix(1)
-        regroup_w_out(S, 1, 256, 320)
+        regroup_w_out(S, 1, 256, 384)
         quantise_w_out(1, 0, 256)
         quantise_hidden(1)
         multiply(1, LEFT)

from contextlib import ExitStack

import concourse.mybir as mybir
from concourse.masks import make_identity

F32 = mybir.dt.float32
BF16 = mybir.dt.bfloat16
U32 = mybir.dt.uint32
U8 = mybir.dt.uint8
FP8X4 = mybir.dt.float8_e4m3fn_x4
ALU = mybir.AluOpType
ACT = mybir.ActivationFunctionType

P = 128
PACK = 4
K_PASS = P * PACK
B, DIM, HID, H, DOUT = 128, 1024, 128, 8, 512
PASSES = DIM // K_PASS
HEADS_PG = H // PASSES
Q = HID // PACK
RUN = 4
HALF = DOUT // 2
LEFT, RIGHT = 0, 1

PER_HEAD = 3
COLUMN_STEP = 16
W_AT, B_AT, DECAY_AT = 0, 1, 2

FLOPS = 2 * B * DIM * H * HID + 2 * B * H * HID * DOUT


def tile_mixedrepeatheads_s_kernel(
    tc, x, index, W_proj, b_proj, W_out, b_out, w_mix, b_mix, decay_values, caches, out
):
    nc = tc.nc
    with ExitStack() as ctx:
        keep = ctx.enter_context(tc.tile_pool(name="keep", bufs=1))
        psum = ctx.enter_context(tc.psum_pool(name="psum", bufs=1))
        ctx.enter_context(tc.manual_schedule())

        bout_all = keep.tile([P, DOUT], BF16)
        vectors = keep.tile([P, DOUT + PER_HEAD * COLUMN_STEP], BF16)
        x_sb = keep.tile([P, DIM], BF16)
        pieces = [(g, c, pair) for g in range(PASSES) for c in range(PASSES) for pair in range(HEADS_PG // 2)]
        wp_rows = {piece: keep.tile([P, 2, PACK, HID], BF16, name="wp_rows%d%d%d" % piece) for piece in pieces}
        caches_sb = [keep.tile([P, HEADS_PG, HID], BF16, name="caches_sb%d" % g) for g in range(PASSES)]
        wo_rows = [keep.tile([P, PACK, DOUT], BF16, name="wo_rows%d" % g) for g in range(PASSES)]

        x_grouped = keep.tile([P, PASSES * B * PACK], BF16, align_bytes=64)
        x_codes = keep.tile([P, PASSES, B], U32, align_bytes=64)
        x_scales = keep.tile([P, PASSES, B], U8, align_bytes=64)
        wp_grouped = [
            keep.tile([P, PASSES, PACK, HEADS_PG, Q, PACK], BF16, name="wp_grouped%d" % g, align_bytes=64)
            for g in range(PASSES)
        ]
        wp_codes = [keep.tile([P, PASSES, PACK, P], U32, name="wp_codes%d" % g, align_bytes=64) for g in range(PASSES)]
        wp_scales = [keep.tile([P, PASSES, PACK, P], U8, name="wp_scales%d" % g, align_bytes=64) for g in range(PASSES)]
        rest = [keep.tile([P, PACK, B], F32, name="rest%d" % g) for g in range(PASSES)]
        hid_grouped = [keep.tile([P, B, PACK], BF16, name="hid_grouped%d" % g, align_bytes=64) for g in range(PASSES)]
        hid_codes = [keep.tile([P, B], U32, name="hid_codes%d" % g, align_bytes=64) for g in range(PASSES)]
        hid_scales = [keep.tile([P, B], U8, name="hid_scales%d" % g, align_bytes=64) for g in range(PASSES)]
        wo_grouped = [keep.tile([P, DOUT, PACK], BF16, name="wo_grouped%d" % g, align_bytes=64) for g in range(PASSES)]
        wo_codes = [keep.tile([P, DOUT], U32, name="wo_codes%d" % g, align_bytes=64) for g in range(PASSES)]
        wo_scales = [keep.tile([P, DOUT], U8, name="wo_scales%d" % g, align_bytes=64) for g in range(PASSES)]
        result = keep.tile([P, DOUT], F32)

        xT = psum.tile([P, PASSES, 2, B], F32, tag="bank_x")
        small_ps = psum.tile([P, PASSES * PER_HEAD + PACK * PASSES], F32)
        bout_ps = psum.tile([P, DOUT], BF16)
        projT = [psum.tile([P, PACK, B], F32, name="projT%d" % g) for g in range(PASSES)]
        acc = [psum.tile([P, HALF], F32, name="acc%d" % half) for half in (LEFT, RIGHT)]

        def regroup_head(copy, piece, head):
            g, c, pair = pieces[piece]
            copy(
                out=wp_grouped[g][:, c, :, 2 * pair + head, :, :].rearrange("p t q j -> p q j t"),
                in_=wp_rows[pieces[piece]][:, head, :, :].rearrange("p j (q t) -> p q j t", t=PACK),
            )

        def quantise_group(g, c):
            nc.vector.quantize_mx(
                out=wp_codes[g][:, c].rearrange("p t m -> p (t m)").bitcast(FP8X4),
                scales=wp_scales[g][:, c].rearrange("p t m -> p (t m)"),
                in_=wp_grouped[g][:, c].rearrange("p t i q j -> p (t i q j)"),
            )

        def project(g):
            for t in range(PACK):
                for c in range(PASSES):
                    nc.tensor.matmul_mx(
                        out=projT[g][:, t, :],
                        lhsT=wp_codes[g][:, c, t, :].bitcast(FP8X4),
                        lhsT_scale=wp_scales[g][:, c, t, :],
                        rhs=x_codes[:, c, :].bitcast(FP8X4),
                        rhs_scale=x_scales[:, c, :],
                        start=(c == 0),
                        stop=(c == PASSES - 1),
                    )

        def prepare_rest(g):
            for u in range(2):
                pair = cachesT[g][:, u, :].bitcast(BF16).rearrange("p (r e) -> p e r", e=2)
                for e in range(2):
                    t = 2 * u + e
                    nc.scalar.activation(
                        out=rest[g][:, t, :], in_=pair[:, e, :],
                        func=ACT.Identity, scale=coef[:, g : g + 1], bias=shift[:, g, t : t + 1],
                    )

        def mix(g):
            nc.vector.scalar_tensor_tensor(
                out=hid_grouped[g][:], in0=projT[g][:].rearrange("p t r -> p r t"), scalar=small[:, g, W_AT : W_AT + 1],
                in1=rest[g][:].rearrange("p t r -> p r t"), op0=ALU.mult, op1=ALU.add,
            )

        def quantise_hidden(g):
            nc.vector.quantize_mx(
                out=hid_codes[g][:].bitcast(FP8X4),
                scales=hid_scales[g][:],
                in_=hid_grouped[g][:].rearrange("p r t -> p (r t)"),
            )

        def regroup_w_out(copy, g, c0, c1):
            copy(
                out=wo_grouped[g][:, c0:c1, :].rearrange("p (a i) j -> p a j i", i=RUN),
                in_=wo_rows[g][:, :, c0:c1].rearrange("p j (a i) -> p a j i", i=RUN),
            )

        def quantise_w_out(g, c0, c1):
            cols = slice(c0, c1)
            nc.vector.quantize_mx(
                out=wo_codes[g][:, cols].bitcast(FP8X4),
                scales=wo_scales[g][:, cols],
                in_=wo_grouped[g][:, cols, :].rearrange("p n j -> p (n j)"),
            )

        def multiply(g, half):
            cols = slice(half * HALF, (half + 1) * HALF)
            nc.tensor.matmul_mx(
                out=acc[half][:],
                lhsT=hid_codes[g][:].bitcast(FP8X4),
                lhsT_scale=hid_scales[g][:],
                rhs=wo_codes[g][:, cols].bitcast(FP8X4),
                rhs_scale=wo_scales[g][:, cols],
                start=(g == 0),
                stop=(g == PASSES - 1),
            )

        def finish(half):
            cols = slice(half * HALF, (half + 1) * HALF)
            nc.vector.tensor_tensor(out=result[:, cols], in0=acc[half][:], in1=bout_all[:, cols], op=ALU.add)
            nc.sync.dma_start(out=out[:, cols], in_=result[:, cols])

        nc.vector.memset(vectors[:].bitcast(F32), 0.0)
        def load_piece(piece):
            g, c, pair = pieces[piece]
            h = HEADS_PG * g + 2 * pair
            nc.sync.dma_start(
                out=wp_rows[pieces[piece]][:].rearrange("p i j n -> p i (j n)"),
                in_=W_proj[h : h + 2, K_PASS * c : K_PASS * (c + 1), :].rearrange("i (p j) n -> p i (j n)", j=PACK),
            )

        for h in range(4):
            load_piece(h)
        per_head_sources = (
            w_mix[:, index : index + 1],
            b_mix[:, index : index + 1],
            decay_values.rearrange("(h o) -> h o", o=1),
        )
        for i in range(PER_HEAD):
            nc.sync.dma_start(
                out=vectors[0:H, DOUT + COLUMN_STEP * i : DOUT + COLUMN_STEP * i + 1], in_=per_head_sources[i]
            )
        load_piece(4)
        nc.sync.dma_start(out=x_sb[:], in_=x)
        load_piece(5)
        nc.sync.dma_start(out=vectors[HEADS_PG : HEADS_PG + PASSES, 0:DOUT], in_=b_proj.rearrange("(g i) k -> g (i k)", g=PASSES))
        nc.sync.dma_start(out=vectors[0:HEADS_PG, 0:DOUT], in_=b_out.partition_broadcast(HEADS_PG))
        load_piece(6)
        load_piece(7)
        wo_view = W_out.rearrange("(g p j) n -> g p (j n)", g=PASSES, p=P, j=PACK)
        nc.sync.dma_start(out=wo_rows[0][:].rearrange("p j n -> p (j n)"), in_=wo_view[0])
        for g in range(PASSES):
            nc.sync.dma_start(
                out=caches_sb[g][:], in_=caches[HEADS_PG * g : HEADS_PG * (g + 1)].rearrange("h r k -> r h k")
            )
        nc.sync.dma_start(out=wo_rows[1][:].rearrange("p j n -> p (j n)"), in_=wo_view[1])

        warm = keep.tile([P, 1], F32)
        nc.vector.memset(warm[:], 1.0)
        nc.scalar.activation(out=warm[:], in_=warm[:], func=ACT.Sqrt)
        select = keep.tile([P, H, Q], BF16)
        nc.gpsimd.memset(select[:], 0.0)
        nc.gpsimd.affine_select(
            out=select[:], in_=select[:], compare_op=ALU.not_equal, fill=1.0,
            base=0, pattern=[[-1, H], [0, Q]], channel_multiplier=1,
        )
        ident = keep.tile([P, P], F32)
        make_identity(nc, ident[:])

        V, S = nc.vector.tensor_copy, nc.scalar.copy
        for n in range(3):
            regroup_head(S, n, 0)
            regroup_head(V, n, 1)
        quantise_group(0, 0)
        regroup_head(S, 3, 0)
        regroup_head(V, 3, 1)
        for g in range(PASSES):
            nc.tensor.matmul(
                small_ps[:, PER_HEAD * g : PER_HEAD * (g + 1)],
                lhsT=select[:, HEADS_PG * g : HEADS_PG * (g + 1), :].rearrange("h n q -> h (n q)"),
                rhs=vectors[:, DOUT : DOUT + PER_HEAD * COLUMN_STEP : COLUMN_STEP],
                start=True,
                stop=True,
            )
        small = keep.tile([P, PASSES, PER_HEAD], F32)
        nc.vector.tensor_copy(out=small[:].rearrange("p g i -> p (g i)"), in_=small_ps[:, 0 : PASSES * PER_HEAD])
        clipped = keep.tile([P, PASSES], F32)
        nc.vector.tensor_scalar(
            out=clipped[:], in0=small[:, :, DECAY_AT], scalar1=0.9, scalar2=1.0, op0=ALU.max, op1=ALU.min,
        )
        coef = keep.tile([P, PASSES], F32)
        shift = keep.tile([P, PASSES, PACK], F32)
        regroup_head(S, 4, 0)
        regroup_head(V, 4, 1)
        quantise_group(0, 1)
        nc.scalar.activation(out=coef[:], in_=clipped[:], func=ACT.Sqrt)
        regroup_head(S, 5, 0)
        regroup_head(V, 5, 1)
        nc.vector.tensor_tensor(out=coef[:, 0:1], in0=coef[:, 0:1], in1=small[:, 0, W_AT : W_AT + 1], op=ALU.mult)

        x_words = x_sb[:].bitcast(F32).rearrange("r (c p u) -> r c u p", c=PASSES, p=P, u=2)
        for c in range(PASSES):
            for u in range(2):
                nc.tensor.transpose(xT[:, c, u, :], x_words[:, c, u, :], ident[:])
        nc.vector.tensor_copy(
            out=x_grouped[:].bitcast(F32).rearrange("p (c r u) -> p c r u", c=PASSES, r=B, u=2),
            in_=xT[:].rearrange("p c u r -> p c r u"),
        )
        regroup_head(V, 6, 1)
        nc.vector.quantize_mx(
            out=x_codes[:].rearrange("p c r -> p (c r)").bitcast(FP8X4),
            scales=x_scales[:].rearrange("p c r -> p (c r)"),
            in_=x_grouped[:],
        )
        regroup_head(S, 6, 0)
        for t in range(PACK):
            at = PASSES * PER_HEAD + PASSES * t
            nc.tensor.matmul(
                small_ps[:, at : at + PASSES],
                lhsT=vectors[:, t:DOUT:PACK],
                rhs=select[:, HEADS_PG : HEADS_PG + PASSES, 0],
                start=True,
                stop=True,
            )
        for repeat in range(2):
            nc.tensor.matmul(
                bout_ps[:], lhsT=select[:, 0:HEADS_PG, :].rearrange("h n q -> h (n q)"), rhs=vectors[:, 0:DOUT],
                start=True, stop=True,
            )
        project(0)
        quantise_group(1, 0)
        bproj = small_ps[:, PASSES * PER_HEAD :].rearrange("p (t g) -> p g t", g=PASSES)
        for g in range(PASSES):
            nc.vector.tensor_scalar(
                out=shift[:, g, :], in0=bproj[:, g, :],
                scalar1=small[:, g, W_AT : W_AT + 1], scalar2=small[:, g, B_AT : B_AT + 1],
                op0=ALU.mult, op1=ALU.add,
            )
        regroup_head(S, 7, 0)
        regroup_head(S, 7, 1)
        quantise_group(1, 1)
        regroup_w_out(S, 0, 0, 256)
        regroup_w_out(V, 0, 256, 512)
        c_words = [
            caches_sb[g][:].rearrange("r h k -> r (h k)").bitcast(F32).rearrange("r (p u) -> r u p", u=2)
            for g in range(PASSES)
        ]
        cachesT = [
            psum.tile([P, 2, B], F32, name="cachesT0", tag="bank_caches"),
            psum.tile([P, 2, B], F32, name="cachesT1", tag="bank_x"),
        ]
        for g in range(PASSES):
            for u in range(2):
                nc.tensor.transpose(cachesT[g][:, u, :], c_words[g][:, u, :], ident[:])
        project(1)
        nc.scalar.copy(out=bout_all[:], in_=bout_ps[:])
        prepare_rest(0)
        prepare_rest(1)
        quantise_w_out(0, 0, 256)
        quantise_w_out(0, 256, 512)
        mix(0)
        regroup_w_out(S, 1, 0, 256)
        regroup_w_out(V, 1, 384, 512)
        quantise_hidden(0)
        multiply(0, LEFT)
        multiply(0, RIGHT)
        mix(1)
        regroup_w_out(S, 1, 256, 384)
        quantise_w_out(1, 0, 256)
        quantise_hidden(1)
        multiply(1, LEFT)
        quantise_w_out(1, 256, 512)
        multiply(1, RIGHT)
        finish(LEFT)
        finish(RIGHT)
